import numpy as np
import ml_dtypes


def mxq(x, axis, fmt="e4m3"):
    dtype, down = {"e4m3": (ml_dtypes.float8_e4m3fn, 7), "e5m2": (ml_dtypes.float8_e5m2, 14)}[fmt]
    v = np.moveaxis(np.asarray(x, np.float32).astype(ml_dtypes.bfloat16).astype(np.float64), axis, -1)
    blocks = v.reshape(v.shape[:-1] + (-1, 32))
    amax = np.abs(blocks).max(-1, keepdims=True)
    byte = np.maximum(np.where(amax > 0, np.frexp(amax)[1] - 1 + 127, 0) - down, 1)
    scale = np.exp2(byte - 127.0)
    codes = (blocks / scale).astype(np.float32).astype(dtype).astype(np.float64)
    return np.moveaxis((codes * scale).reshape(v.shape), -1, axis)


WIDE = False


def mx_kscale(k):
    if not WIDE:
        return np.ones(k)
    levels = np.array([10, -10, 5, -5, 0])
    a = np.random.permutation(np.resize(levels, k // 512 * 4)).reshape(k // 512, 4)
    idx = np.arange(k)
    return np.exp2(a[idx // 512, idx % 128 // 32])


BF16 = ml_dtypes.bfloat16


def bf(x):
    return np.asarray(x, np.float32).astype(BF16)


def f64(x):
    return np.asarray(x).astype(np.float64)


M, K, N = 4096, 512, 1024

EPS = 1e-08


def setup_inputs():
    limit = np.sqrt(6.0 / (K + N))
    s = mx_kscale(K)
    g = np.exp2(np.round(np.log2(s.max() / s.min()) / 4))
    return {"x": bf(np.random.standard_normal((M, K)) * s[None, :]),
            "weight": bf(np.random.uniform(-limit, limit, (N, K)) / s[None, :] * g),
            "mask": bf((np.random.random((N, K)) < 0.8).astype(np.float64)),
            "bias": bf(np.random.standard_normal(N) * 0.1)}


def reference(x, weight, mask, bias):
    mw = f64(weight) * f64(mask)
    aw = np.abs(mw)
    scale = aw.mean() + EPS
    threshold = np.std(aw, ddof=1) * 0.5
    tern = np.where(mw > threshold, 1.0, 0.0) + np.where(mw < -threshold, -1.0, 0.0)
    tw = tern * scale
    return (mxq(f64(x), 1, "e4m3") @ mxq(tw, 1, "e4m3").T) + f64(bias)

@@ -1,0 +1,252 @@
+from contextlib import ExitStack
+
+import concourse.mybir as mybir
+from concourse.masks import make_identity
+
+FP8X4 = mybir.dt.float8_e4m3fn_x4
+BF16 = mybir.dt.bfloat16
+F32 = mybir.dt.float32
+U32 = mybir.dt.uint32
+U8 = mybir.dt.uint8
+ALU = mybir.AluOpType
+ACT = mybir.ActivationFunctionType
+AXIS = mybir.AxisListType
+
+P = 128
+M, K, N = 4096, 512, 1024
+EPS = 1e-08
+COUNT = N * K
+FLOPS = 2 * M * K * N
+
+MT = M // P
+WT = N // P
+XCH = 4
+TPC = MT // XCH
+MANUAL = False
+GROUPS = [1, 1, 2, 4, 4, 4, 4, 4, 4, 2, 1, 1]
+
+
+def on_scalar_and_gpsimd(t, h):
+    return (2 * t + h) % 4 == 1 and t < MT - 2
+
+
+def tile_masklockedlinear_t_kernel(tc, x, weight, mask, bias, out):
+    nc = tc.nc
+    with ExitStack() as ctx:
+        if MANUAL:
+            ctx.enter_context(tc.manual_schedule())
+        const = ctx.enter_context(tc.tile_pool(name="const", bufs=1))
+        outp = ctx.enter_context(tc.tile_pool(name="outp", bufs=4))
+        tp = ctx.enter_context(tc.psum_pool(name="tp", bufs=3))
+        accp = ctx.enter_context(tc.psum_pool(name="accp", bufs=4))
+        misc = ctx.enter_context(tc.psum_pool(name="misc", bufs=1))
+
+        one_col = const.tile([P, 1], F32, name="one_col")
+        nc.vector.memset(one_col[:], 1.0)
+        warm = const.tile([P, 1], F32, name="warm")
+        nc.scalar.activation(out=warm[:], in_=one_col[:], func=ACT.Sqrt)
+        ident = const.tile([P, P], F32, name="ident")
+        make_identity(nc, ident[:])
+        bias_row = const.tile([P, N], BF16, name="bias_row")
+        nc.vector.memset(bias_row[:], 0.0)
+        ones_b = const.tile([P, P], BF16, name="ones_b")
+        nc.vector.memset(ones_b[:], 1.0)
+        ones_f = const.tile([P, P], F32, name="ones_f")
+        nc.vector.memset(ones_f[:], 1.0)
+        stats = const.tile([P, 16], F32, name="stats")
+        nc.vector.memset(stats[:], 0.0)
+
+        nc.scalar.dma_start(out=bias_row[0:1, :], in_=bias.rearrange("(o n) -> o n", o=1))
+        w_v = weight.rearrange("(p t) k -> p t k", t=WT)
+        m_v = mask.rearrange("(p t) k -> p t k", t=WT)
+        x_v = x.rearrange("(p t) k -> p t k", t=MT)
+        out_v = out.rearrange("(p t) n -> p t n", t=MT)
+        w_sb, m_sb = [], []
+        for c in range(4):
+            w_c = const.tile([P, 2, K], BF16, name="w%d" % c)
+            nc.sync.dma_start(out=w_c[:], in_=w_v[:, 2 * c : 2 * c + 2, :])
+            m_c = const.tile([P, 2, K], BF16, name="m%d" % c)
+            nc.sync.dma_start(out=m_c[:], in_=m_v[:, 2 * c : 2 * c + 2, :])
+            w_sb.append(w_c)
+            m_sb.append(m_c)
+        x_sb = []
+        for j in range(XCH):
+            x_c = const.tile([P, TPC * K], BF16, name="x%d" % j)
+            nc.sync.dma_start(
+                out=x_c[:].rearrange("p (t k) -> p t k", t=TPC),
+                in_=x_v[:, TPC * j : TPC * j + TPC, :],
+            )
+            x_sb.append(x_c)
+
+        bias_sb = const.tile([P, N], F32, name="bias_sb")
+        for h in range(2):
+            cols = slice(512 * h, 512 * h + 512)
+            pb = accp.tile([P, 512], F32, name="pb", tag="acc")
+            nc.tensor.matmul(pb[:], lhsT=ones_b[:], rhs=bias_row[:, cols], start=True, stop=True)
+            nc.scalar.copy(out=bias_sb[:, cols], in_=pb[:])
+
+        mwT = const.tile([P, 4 * N], BF16, name="mwT", align_bytes=64)
+        mwT32 = mwT[:].bitcast(F32).rearrange("q (p t u) -> q p t u", p=P, t=WT, u=2)
+        junk = const.tile([P, 2, K], BF16, name="junk")
+        gram = misc.tile([P, P], F32, name="gram", tag="misc")
+        pts = []
+        for c in range(4):
+            mw_c = const.tile([P, 2, K], BF16, name="mw%d" % c)
+            nc.vector.tensor_tensor(out=mw_c[:], in0=w_sb[c][:], in1=m_sb[c][:], op=ALU.mult)
+            nc.scalar.activation(
+                out=junk[:], in_=mw_c[:], func=ACT.Abs, accum_out=stats[:, c : c + 1]
+            )
+            for a in range(2):
+                for b in range(4):
+                    blk = mw_c[:, a, P * b : P * b + P]
+                    nc.tensor.matmul(
+                        gram[:],
+                        lhsT=blk,
+                        rhs=blk,
+                        start=(c == 0 and a == 0 and b == 0),
+                        stop=(c == 3 and a == 1 and b == 3),
+                    )
+            mw32 = mw_c[:].rearrange("p t k -> p (t k)").bitcast(F32)
+            pt = accp.tile([P, 2, 2, P], F32, name="pt", tag="acc")
+            for a in range(2):
+                for u in range(2):
+                    o = 256 * a + P * u
+                    nc.tensor.transpose(pt[:, a, u, :], mw32[:, o : o + P], ident[:])
+            pts.append(pt)
+        for c in range(4):
+            src = pts[c][:].rearrange("q a u p -> q p a u")
+            dst = mwT32[:, :, 2 * c : 2 * c + 2, :]
+            if c < 2:
+                nc.vector.tensor_copy(out=dst, in_=src)
+            else:
+                nc.scalar.copy(out=dst, in_=src)
+
+        diag = const.tile([P, P], F32, name="diag")
+        nc.vector.scalar_tensor_tensor(
+            out=diag[:], in0=gram[:], scalar=1.0, in1=ident[:],
+            op0=ALU.mult, op1=ALU.mult, accum_out=stats[:, 8:9],
+        )
+        tot = misc.tile([P, 16], F32, name="tot", tag="misc")
+        nc.tensor.matmul(tot[:], lhsT=ones_f[:], rhs=stats[:], start=True, stop=True)
+
+        s1 = const.tile([P, 1], F32, name="s1")
+        nc.vector.tensor_reduce(out=s1[:], in_=tot[:, 0:4], axis=AXIS.X, op=ALU.add)
+        sq = const.tile([P, 1], F32, name="sq")
+        nc.vector.scalar_tensor_tensor(
+            out=sq[:], in0=s1[:], scalar=1.0 / (4.0 * COUNT * (COUNT - 1.0)), in1=s1[:],
+            op0=ALU.mult, op1=ALU.mult,
+        )
+        var4 = const.tile([P, 1], F32, name="var4")
+        nc.vector.scalar_tensor_tensor(
+            out=var4[:], in0=tot[:, 8:9], scalar=1.0 / (4.0 * (COUNT - 1.0)), in1=sq[:],
+            op0=ALU.mult, op1=ALU.subtract,
+        )
+        var4p = const.tile([P, 1], F32, name="var4p")
+        nc.vector.tensor_scalar_max(out=var4p[:], in0=var4[:], scalar1=0.0)
+        thr = const.tile([P, 1], F32, name="thr")
+        nc.scalar.activation(out=thr[:], in_=var4p[:], func=ACT.Sqrt)
+        nthr = const.tile([P, 1], F32, name="nthr")
+        nc.scalar.mul(out=nthr[:], in_=thr[:], mul=-1.0)
+        scl = const.tile([P, 1], F32, name="scl")
+        nc.vector.tensor_scalar(
+            out=scl[:], in0=s1[:], scalar1=1.0 / COUNT, scalar2=EPS, op0=ALU.mult, op1=ALU.add
+        )
+
+        xg, xc, xs = [], [], []
+        for j in range(XCH):
+            xg.append(const.tile([P, TPC * K], BF16, name="xg%d" % j, align_bytes=64))
+            xc.append(const.tile([P, TPC * P], U32, name="xc%d" % j, align_bytes=64))
+            xs.append(const.tile([P, TPC * P], U8, name="xs%d" % j, align_bytes=64))
+
+        def x_bank(j, b):
+            x32 = x_sb[j][:].bitcast(F32)
+            xt = tp.tile([P, 2, 2, P], F32, name="xt", tag="tp")
+            for a in range(2):
+                for u in range(2):
+                    o = 256 * (2 * b + a) + P * u
+                    nc.tensor.transpose(xt[:, a, u, :], x32[:, o : o + P], ident[:])
+            dst = xg[j][:].bitcast(F32)[:, 512 * b : 512 * b + 512]
+            nc.scalar.copy(
+                out=dst.rearrange("q (a p u) -> q a p u", a=2, p=P, u=2),
+                in_=xt[:].rearrange("q a u p -> q a p u"),
+            )
+
+        def x_quant(j, b0, nb):
+            nc.vector.quantize_mx(
+                out=xc[j][:, 256 * b0 : 256 * (b0 + nb)].bitcast(FP8X4),
+                scales=xs[j][:, 256 * b0 : 256 * (b0 + nb)],
+                in_=xg[j][:, 1024 * b0 : 1024 * (b0 + nb)],
+            )
+
+        for b in range(4):
+            x_bank(0, b)
+
+        tw = const.tile([P, 4 * N], BF16, name="tw", align_bytes=64)
+        neg = const.tile([P, 4 * N], BF16, name="neg")
+        twc = const.tile([P, N], U32, name="twc", align_bytes=64)
+        tws = const.tile([P, N], U8, name="tws", align_bytes=64)
+
+        def tern(h):
+            cols = slice(2048 * h, 2048 * h + 2048)
+            nc.vector.tensor_scalar(
+                out=tw[:, cols], in0=mwT[:, cols], scalar1=thr[:, 0:1], scalar2=scl[:, 0:1],
+                op0=ALU.is_gt, op1=ALU.mult,
+            )
+            nc.vector.tensor_scalar(
+                out=neg[:, cols], in0=mwT[:, cols], scalar1=nthr[:, 0:1], scalar2=scl[:, 0:1],
+                op0=ALU.is_lt, op1=ALU.mult,
+            )
+            nc.vector.tensor_tensor(
+                out=tw[:, cols], in0=tw[:, cols], in1=neg[:, cols], op=ALU.subtract
+            )
+
+        def tw_quant(h):
+            nc.vector.quantize_mx(
+                out=twc[:, 512 * h : 512 * h + 512].bitcast(FP8X4),
+                scales=tws[:, 512 * h : 512 * h + 512],
+                in_=tw[:, 2048 * h : 2048 * h + 2048],
+            )
+
+        tern(0)
+        x_quant(0, 0, 1)
+        tw_quant(0)
+        tern(1)
+        x_quant(0, 1, 1)
+        tw_quant(1)
+        x_quant(0, 2, 2)
+
+        t = 0
+        for g in GROUPS:
+            ob = outp.tile([P, 4, N], F32, name="ob", tag="ob")
+            for i in range(g):
+                j, tl = divmod(t + i, TPC)
+                for h in range(2):
+                    cols = slice(512 * h, 512 * h + 512)
+                    acc = accp.tile([P, 512], F32, name="acc", tag="acc")
+                    nc.tensor.matmul_mx(
+                        out=acc[:],
+                        lhsT=xc[j][:, P * tl : P * tl + P].bitcast(FP8X4),
+                        lhsT_scale=xs[j][:, P * tl : P * tl + P],
+                        rhs=twc[:, cols].bitcast(FP8X4),
+                        rhs_scale=tws[:, cols],
+                        start=True,
+                        stop=True,
+                    )
+                    if on_scalar_and_gpsimd(t + i, h):
+                        nc.scalar.copy(out=ob[:, i, cols], in_=acc[:])
+                        nc.gpsimd.tensor_tensor(
+                            out=ob[:, i, cols], in0=ob[:, i, cols], in1=bias_sb[:, cols], op=ALU.add
+                        )
+                    else:
+                        nc.vector.tensor_tensor(
+                            out=ob[:, i, cols], in0=acc[:], in1=bias_sb[:, cols], op=ALU.add
+                        )
+                tt = t + i
+                if tt % 4 == 3 and tt // TPC + 1 < XCH:
+                    jn = tt // TPC + 1
+                    b0 = 2 * ((tt % TPC) // 4)
+                    x_bank(jn, b0)
+                    x_bank(jn, b0 + 1)
+                    x_quant(jn, b0, 2)
+            nc.sync.dma_start(out=out_v[:, t : t + g, :], in_=ob[:, 0:g, :])
+            t += g

@@ -22,53 +22,55 @@ MT = M // P
 WT = N // P
 XCH = 4
 TPC = MT // XCH
-MANUAL = False
-GROUPS = [1, 1, 2, 4, 4, 4, 4, 4, 4, 2, 1, 1]
+GROUPS = [1, 1, 1, 1, 2, 2, 2, 2, 4, 4, 4, 4, 2, 1, 1]
+OB_BUFS = {1: 4, 2: 4, 4: 3}
+EARLY = 3
 
 
 def on_scalar_and_gpsimd(t, h):
-    return (2 * t + h) % 4 == 1 and t < MT - 2
+    if t < EARLY:
+        return h == 0
+    return (2 * t + h) % 16 in (1, 4, 7, 10, 13) and t < MT - 2
 
 
 def tile_masklockedlinear_t_kernel(tc, x, weight, mask, bias, out):
     nc = tc.nc
     with ExitStack() as ctx:
-        if MANUAL:
-            ctx.enter_context(tc.manual_schedule())
+        ctx.enter_context(tc.manual_schedule())
         const = ctx.enter_context(tc.tile_pool(name="const", bufs=1))
-        outp = ctx.enter_context(tc.tile_pool(name="outp", bufs=4))
+        outp = ctx.enter_context(tc.tile_pool(name="outp", bufs=1))
+        xgp = ctx.enter_context(tc.tile_pool(name="xgp", bufs=2))
         tp = ctx.enter_context(tc.psum_pool(name="tp", bufs=3))
-        accp = ctx.enter_context(tc.psum_pool(name="accp", bufs=4))
-        misc = ctx.enter_context(tc.psum_pool(name="misc", bufs=1))
+        accp = ctx.enter_context(tc.psum_pool(name="accp", bufs=5))
 
+        bias_row = const.tile([P, N], BF16, name="bias_row")
+        nc.vector.memset(bias_row[:], 0.0)
         one_col = const.tile([P, 1], F32, name="one_col")
         nc.vector.memset(one_col[:], 1.0)
         warm = const.tile([P, 1], F32, name="warm")
         nc.scalar.activation(out=warm[:], in_=one_col[:], func=ACT.Sqrt)
         ident = const.tile([P, P], F32, name="ident")
         make_identity(nc, ident[:])
-        bias_row = const.tile([P, N], BF16, name="bias_row")
-        nc.vector.memset(bias_row[:], 0.0)
         ones_b = const.tile([P, P], BF16, name="ones_b")
         nc.vector.memset(ones_b[:], 1.0)
         ones_f = const.tile([P, P], F32, name="ones_f")
         nc.vector.memset(ones_f[:], 1.0)
-        stats = const.tile([P, 16], F32, name="stats")
+        stats = const.tile([P, 40], F32, name="stats")
         nc.vector.memset(stats[:], 0.0)
 
-        nc.scalar.dma_start(out=bias_row[0:1, :], in_=bias.rearrange("(o n) -> o n", o=1))
-        w_v = weight.rearrange("(p t) k -> p t k", t=WT)
-        m_v = mask.rearrange("(p t) k -> p t k", t=WT)
+        w_v = weight.rearrange("(c p a) k -> c p a k", c=4, p=P, a=2)
+        m_v = mask.rearrange("(c p a) k -> c p a k", c=4, p=P, a=2)
         x_v = x.rearrange("(p t) k -> p t k", t=MT)
         out_v = out.rearrange("(p t) n -> p t n", t=MT)
         w_sb, m_sb = [], []
         for c in range(4):
             w_c = const.tile([P, 2, K], BF16, name="w%d" % c)
-            nc.sync.dma_start(out=w_c[:], in_=w_v[:, 2 * c : 2 * c + 2, :])
+            nc.sync.dma_start(out=w_c[:], in_=w_v[c])
             m_c = const.tile([P, 2, K], BF16, name="m%d" % c)
-            nc.sync.dma_start(out=m_c[:], in_=m_v[:, 2 * c : 2 * c + 2, :])
+            nc.sync.dma_start(out=m_c[:], in_=m_v[c])
             w_sb.append(w_c)
             m_sb.append(m_c)
+        nc.sync.dma_start(out=bias_row[0:1, :], in_=bias.rearrange("(o n) -> o n", o=1))
         x_sb = []
         for j in range(XCH):
             x_c = const.tile([P, TPC * K], BF16, name="x%d" % j)
@@ -78,23 +80,41 @@ def tile_masklockedlinear_t_kernel(tc, x, weight, mask, bias, out):
             )
             x_sb.append(x_c)
 
-        bias_sb = const.tile([P, N], F32, name="bias_sb")
-        for h in range(2):
-            cols = slice(512 * h, 512 * h + 512)
-            pb = accp.tile([P, 512], F32, name="pb", tag="acc")
-            nc.tensor.matmul(pb[:], lhsT=ones_b[:], rhs=bias_row[:, cols], start=True, stop=True)
-            nc.scalar.copy(out=bias_sb[:, cols], in_=pb[:])
-
         mwT = const.tile([P, 4 * N], BF16, name="mwT", align_bytes=64)
-        mwT32 = mwT[:].bitcast(F32).rearrange("q (p t u) -> q p t u", p=P, t=WT, u=2)
+        mwT32 = mwT[:].bitcast(F32).rearrange("q (c p a u) -> q c p a u", c=4, p=P, a=2, u=2)
         junk = const.tile([P, 2, K], BF16, name="junk")
-        gram = misc.tile([P, P], F32, name="gram", tag="misc")
-        pts = []
+        gram = tp.tile([P, P], F32, name="gram", tag="tp")
+        tot = tp.tile([P, 2], F32, name="tot", tag="tp")
+
+        def stat_mm(i, first, last):
+            nc.tensor.matmul(
+                tot[:], lhsT=ones_f[:], rhs=stats[:, 8 * i : 8 * i + 2], start=first, stop=last
+            )
+
+        mws, pts = [], {}
+
+        def mw_transposes(c):
+            mw32 = mws[c][:].rearrange("p t k -> p (t k)").bitcast(F32)
+            pt = accp.tile([P, 2, 2, P], F32, name="pt", tag="acc")
+            for a in range(2):
+                for u in range(2):
+                    o = 256 * a + P * u
+                    nc.tensor.transpose(pt[:, a, u, :], mw32[:, o : o + P], ident[:])
+            pts[c] = pt
+
+        def mw_exit(c, engine):
+            src = pts[c][:].rearrange("q a u p -> q p a u")
+            if engine == "v":
+                nc.vector.tensor_copy(out=mwT32[:, c], in_=src)
+            else:
+                nc.scalar.copy(out=mwT32[:, c], in_=src)
+
         for c in range(4):
             mw_c = const.tile([P, 2, K], BF16, name="mw%d" % c)
+            mws.append(mw_c)
             nc.vector.tensor_tensor(out=mw_c[:], in0=w_sb[c][:], in1=m_sb[c][:], op=ALU.mult)
             nc.scalar.activation(
-                out=junk[:], in_=mw_c[:], func=ACT.Abs, accum_out=stats[:, c : c + 1]
+                out=junk[:], in_=mw_c[:], func=ACT.Abs, accum_out=stats[:, 8 * c : 8 * c + 1]
             )
             for a in range(2):
                 for b in range(4):
@@ -106,65 +126,58 @@ def tile_masklockedlinear_t_kernel(tc, x, weight, mask, bias, out):
                         start=(c == 0 and a == 0 and b == 0),
                         stop=(c == 3 and a == 1 and b == 3),
                     )
-            mw32 = mw_c[:].rearrange("p t k -> p (t k)").bitcast(F32)
-            pt = accp.tile([P, 2, 2, P], F32, name="pt", tag="acc")
-            for a in range(2):
-                for u in range(2):
-                    o = 256 * a + P * u
-                    nc.tensor.transpose(pt[:, a, u, :], mw32[:, o : o + P], ident[:])
-            pts.append(pt)
-        for c in range(4):
-            src = pts[c][:].rearrange("q a u p -> q p a u")
-            dst = mwT32[:, :, 2 * c : 2 * c + 2, :]
             if c < 2:
-                nc.vector.tensor_copy(out=dst, in_=src)
-            else:
-                nc.scalar.copy(out=dst, in_=src)
-
+                mw_transposes(c)
+        for c in range(3):
+            stat_mm(c, c == 0, False)
+        mw_exit(0, "v")
         diag = const.tile([P, P], F32, name="diag")
         nc.vector.scalar_tensor_tensor(
-            out=diag[:], in0=gram[:], scalar=1.0, in1=ident[:],
-            op0=ALU.mult, op1=ALU.mult, accum_out=stats[:, 8:9],
+            out=diag[:], in0=gram[:], scalar=float(COUNT), in1=ident[:],
+            op0=ALU.mult, op1=ALU.mult, accum_out=stats[:, 33:34],
         )
-        tot = misc.tile([P, 16], F32, name="tot", tag="misc")
-        nc.tensor.matmul(tot[:], lhsT=ones_f[:], rhs=stats[:], start=True, stop=True)
+        mw_exit(1, "v")
+        stat_mm(4, False, False)
+        stat_mm(3, False, True)
 
-        s1 = const.tile([P, 1], F32, name="s1")
-        nc.vector.tensor_reduce(out=s1[:], in_=tot[:, 0:4], axis=AXIS.X, op=ALU.add)
-        sq = const.tile([P, 1], F32, name="sq")
-        nc.vector.scalar_tensor_tensor(
-            out=sq[:], in0=s1[:], scalar=1.0 / (4.0 * COUNT * (COUNT - 1.0)), in1=s1[:],
-            op0=ALU.mult, op1=ALU.mult,
-        )
-        var4 = const.tile([P, 1], F32, name="var4")
-        nc.vector.scalar_tensor_tensor(
-            out=var4[:], in0=tot[:, 8:9], scalar=1.0 / (4.0 * (COUNT - 1.0)), in1=sq[:],
+        nv = const.tile([P, 1], F32, name="nv")
+        nc.vector.tensor_scalar(
+            out=nv[:], in0=tot[:, 0:1], scalar1=tot[:, 0:1], scalar2=tot[:, 1:2],
             op0=ALU.mult, op1=ALU.subtract,
         )
-        var4p = const.tile([P, 1], F32, name="var4p")
-        nc.vector.tensor_scalar_max(out=var4p[:], in0=var4[:], scalar1=0.0)
+        nvc = const.tile([P, 1], F32, name="nvc")
+        nc.vector.tensor_scalar_min(out=nvc[:], in0=nv[:], scalar1=0.0)
         thr = const.tile([P, 1], F32, name="thr")
-        nc.scalar.activation(out=thr[:], in_=var4p[:], func=ACT.Sqrt)
+        nc.scalar.activation(
+            out=thr[:], in_=nvc[:], func=ACT.Sqrt, scale=-1.0 / (4.0 * COUNT * (COUNT - 1.0))
+        )
         nthr = const.tile([P, 1], F32, name="nthr")
         nc.scalar.mul(out=nthr[:], in_=thr[:], mul=-1.0)
         scl = const.tile([P, 1], F32, name="scl")
         nc.vector.tensor_scalar(
-            out=scl[:], in0=s1[:], scalar1=1.0 / COUNT, scalar2=EPS, op0=ALU.mult, op1=ALU.add
+            out=scl[:], in0=tot[:, 0:1], scalar1=1.0 / COUNT, scalar2=EPS, op0=ALU.mult, op1=ALU.add
         )
 
-        xg, xc, xs = [], [], []
+        xg, xc, xs = {}, [], []
         for j in range(XCH):
-            xg.append(const.tile([P, TPC * K], BF16, name="xg%d" % j, align_bytes=64))
             xc.append(const.tile([P, TPC * P], U32, name="xc%d" % j, align_bytes=64))
             xs.append(const.tile([P, TPC * P], U8, name="xs%d" % j, align_bytes=64))
 
-        def x_bank(j, b):
+        xts = {}
+
+        def x_bank_t(j, b):
             x32 = x_sb[j][:].bitcast(F32)
             xt = tp.tile([P, 2, 2, P], F32, name="xt", tag="tp")
             for a in range(2):
                 for u in range(2):
                     o = 256 * (2 * b + a) + P * u
                     nc.tensor.transpose(xt[:, a, u, :], x32[:, o : o + P], ident[:])
+            xts[(j, b)] = xt
+
+        def x_bank_s(j, b):
+            xt = xts[(j, b)]
+            if j not in xg:
+                xg[j] = xgp.tile([P, TPC * K], BF16, name="xg", tag="xg", align_bytes=64)
             dst = xg[j][:].bitcast(F32)[:, 512 * b : 512 * b + 512]
             nc.scalar.copy(
                 out=dst.rearrange("q (a p u) -> q a p u", a=2, p=P, u=2),
@@ -178,11 +191,38 @@ def tile_masklockedlinear_t_kernel(tc, x, weight, mask, bias, out):
                 in_=xg[j][:, 1024 * b0 : 1024 * (b0 + nb)],
             )
 
-        for b in range(4):
-            x_bank(0, b)
+        def x_pair(i):
+            for b in (2 * (i % 2), 2 * (i % 2) + 1):
+                x_bank_t(1 + i // 2, b)
+                x_bank_s(1 + i // 2, b)
+
+        bias_sb = const.tile([P, N], F32, name="bias_sb")
+        pbs = {}
+
+        def bias_t(h):
+            pb = accp.tile([P, 512], F32, name="pb", tag="acc")
+            nc.tensor.matmul(
+                pb[:], lhsT=ones_b[:], rhs=bias_row[:, 512 * h : 512 * h + 512], start=True, stop=True
+            )
+            pbs[h] = pb
+
+        def bias_s(h):
+            nc.scalar.copy(out=bias_sb[:, 512 * h : 512 * h + 512], in_=pbs[h][:])
+
+        x_bank_t(0, 0)
+        x_bank_t(0, 1)
+        mw_transposes(2)
+        mw_transposes(3)
+        bias_t(0)
+        bias_t(1)
+        x_bank_s(0, 0)
+        x_bank_s(0, 1)
+        mw_exit(2, "s")
+        mw_exit(3, "s")
+        bias_s(0)
 
         tw = const.tile([P, 4 * N], BF16, name="tw", align_bytes=64)
-        neg = const.tile([P, 4 * N], BF16, name="neg")
+        neg = const.tile([P, 2 * N], BF16, name="neg")
         twc = const.tile([P, N], U32, name="twc", align_bytes=64)
         tws = const.tile([P, N], U8, name="tws", align_bytes=64)
 
@@ -193,11 +233,11 @@ def tile_masklockedlinear_t_kernel(tc, x, weight, mask, bias, out):
                 op0=ALU.is_gt, op1=ALU.mult,
             )
             nc.vector.tensor_scalar(
-                out=neg[:, cols], in0=mwT[:, cols], scalar1=nthr[:, 0:1], scalar2=scl[:, 0:1],
+                out=neg[:], in0=mwT[:, cols], scalar1=nthr[:, 0:1], scalar2=scl[:, 0:1],
                 op0=ALU.is_lt, op1=ALU.mult,
             )
             nc.vector.tensor_tensor(
-                out=tw[:, cols], in0=tw[:, cols], in1=neg[:, cols], op=ALU.subtract
+                out=tw[:, cols], in0=tw[:, cols], in1=neg[:], op=ALU.subtract
             )
 
         def tw_quant(h):
@@ -207,46 +247,72 @@ def tile_masklockedlinear_t_kernel(tc, x, weight, mask, bias, out):
                 in_=tw[:, 2048 * h : 2048 * h + 2048],
             )
 
+        obs = {}
+        first_of = {}
+        size_of = {}
+        t0 = 0
+        for g in GROUPS:
+            for i in range(g):
+                first_of[t0 + i] = t0
+            size_of[t0] = g
+            t0 += g
+
+        def unit(t, h):
+            f = first_of[t]
+            if f not in obs:
+                g = size_of[f]
+                obs[f] = outp.tile([P, g, N], F32, name="ob%d" % g, tag="ob%d" % g, bufs=OB_BUFS[g])
+            ob = obs[f]
+            i = t - f
+            j, tl = divmod(t, TPC)
+            cols = slice(512 * h, 512 * h + 512)
+            acc = accp.tile([P, 512], F32, name="acc", tag="acc")
+            nc.tensor.matmul_mx(
+                out=acc[:],
+                lhsT=xc[j][:, P * tl : P * tl + P].bitcast(FP8X4),
+                lhsT_scale=xs[j][:, P * tl : P * tl + P],
+                rhs=twc[:, cols].bitcast(FP8X4),
+                rhs_scale=tws[:, cols],
+                start=True,
+                stop=True,
+            )
+            if on_scalar_and_gpsimd(t, h):
+                nc.scalar.copy(out=ob[:, i, cols], in_=acc[:])
+                nc.gpsimd.tensor_tensor(
+                    out=ob[:, i, cols], in0=ob[:, i, cols], in1=bias_sb[:, cols], op=ALU.add
+                )
+            else:
+                nc.vector.tensor_tensor(
+                    out=ob[:, i, cols], in0=acc[:], in1=bias_sb[:, cols], op=ALU.add
+                )
+
         tern(0)
         x_quant(0, 0, 1)
         tw_quant(0)
-        tern(1)
         x_quant(0, 1, 1)
+        unit(0, 0)
+        bias_s(1)
+        for t in range(1, EARLY):
+            unit(t, 0)
+        for b in (2, 3):
+            x_bank_t(0, b)
+            x_bank_s(0, b)
+        tern(1)
         tw_quant(1)
-        x_quant(0, 2, 2)
 
-        t = 0
-        for g in GROUPS:
-            ob = outp.tile([P, 4, N], F32, name="ob", tag="ob")
-            for i in range(g):
-                j, tl = divmod(t + i, TPC)
-                for h in range(2):
-                    cols = slice(512 * h, 512 * h + 512)
-                    acc = accp.tile([P, 512], F32, name="acc", tag="acc")
-                    nc.tensor.matmul_mx(
-                        out=acc[:],
-                        lhsT=xc[j][:, P * tl : P * tl + P].bitcast(FP8X4),
-                        lhsT_scale=xs[j][:, P * tl : P * tl + P],
-                        rhs=twc[:, cols].bitcast(FP8X4),
-                        rhs_scale=tws[:, cols],
-                        start=True,
-                        stop=True,
-                    )
-                    if on_scalar_and_gpsimd(t + i, h):
-                        nc.scalar.copy(out=ob[:, i, cols], in_=acc[:])
-                        nc.gpsimd.tensor_tensor(
-                            out=ob[:, i, cols], in0=ob[:, i, cols], in1=bias_sb[:, cols], op=ALU.add
-                        )
-                    else:
-                        nc.vector.tensor_tensor(
-                            out=ob[:, i, cols], in0=acc[:], in1=bias_sb[:, cols], op=ALU.add
-                        )
-                tt = t + i
-                if tt % 4 == 3 and tt // TPC + 1 < XCH:
-                    jn = tt // TPC + 1
-                    b0 = 2 * ((tt % TPC) // 4)
-                    x_bank(jn, b0)
-                    x_bank(jn, b0 + 1)
-                    x_quant(jn, b0, 2)
-            nc.sync.dma_start(out=out_v[:, t : t + g, :], in_=ob[:, 0:g, :])
-            t += g
+        for t in range(MT):
+            if t >= EARLY:
+                unit(t, 0)
+            unit(t, 1)
+            f = first_of[t]
+            if t == f + size_of[f] - 1:
+                g = size_of[f]
+                nc.sync.dma_start(out=out_v[:, f : f + g, :], in_=obs[f][:, 0:g, :])
+            if t == 1:
+                x_quant(0, 2, 2)
+                x_pair(0)
+            if t % 4 == 3 and t // 4 + 1 < 6:
+                x_pair(t // 4 + 1)
+            if t == 3 or (t % 4 == 1 and 1 <= t // 4 < 6):
+                i = t // 4 if t != 3 else 0
+                x_quant(1 + i // 2, 2 * (i % 2), 2)

@@ -30,7 +30,7 @@ EARLY = 3
 def on_scalar_and_gpsimd(t, h):
     if t < EARLY:
         return h == 0
-    return (2 * t + h) % 16 in (1, 4, 7, 10, 13) and t < MT - 2
+    return (2 * t + h) % 8 in (1, 4, 6) and t < MT - 2
 
 
 def tile_masklockedlinear_t_kernel(tc, x, weight, mask, bias, out):

@@ -24,13 +24,15 @@ XCH = 4
 TPC = MT // XCH
 GROUPS = [1, 1, 1, 1, 2, 2, 2, 2, 4, 4, 4, 4, 2, 1, 1]
 OB_BUFS = {1: 4, 2: 4, 4: 3}
+CHUNKS = [(0, 2), (256, 2), (512, 2), (768, 1), (896, 1)]
+NCH = len(CHUNKS)
 EARLY = 3
 
 
 def on_scalar_and_gpsimd(t, h):
     if t < EARLY:
         return h == 0
-    return (2 * t + h) % 8 in (1, 4, 6) and t < MT - 2
+    return (2 * t + h) % 16 in (1, 4, 7, 10, 13) and t < MT - 2
 
 
 def tile_masklockedlinear_t_kernel(tc, x, weight, mask, bias, out):
@@ -55,19 +57,22 @@ def tile_masklockedlinear_t_kernel(tc, x, weight, mask, bias, out):
         nc.vector.memset(ones_b[:], 1.0)
         ones_f = const.tile([P, P], F32, name="ones_f")
         nc.vector.memset(ones_f[:], 1.0)
-        stats = const.tile([P, 40], F32, name="stats")
+        stats = const.tile([P, 16], F32, name="stats")
         nc.vector.memset(stats[:], 0.0)
 
-        w_v = weight.rearrange("(c p a) k -> c p a k", c=4, p=P, a=2)
-        m_v = mask.rearrange("(c p a) k -> c p a k", c=4, p=P, a=2)
         x_v = x.rearrange("(p t) k -> p t k", t=MT)
         out_v = out.rearrange("(p t) n -> p t n", t=MT)
         w_sb, m_sb = [], []
-        for c in range(4):
-            w_c = const.tile([P, 2, K], BF16, name="w%d" % c)
-            nc.sync.dma_start(out=w_c[:], in_=w_v[c])
-            m_c = const.tile([P, 2, K], BF16, name="m%d" % c)
-            nc.sync.dma_start(out=m_c[:], in_=m_v[c])
+        for c in range(NCH):
+            r0, na = CHUNKS[c]
+            w_c = const.tile([P, na, K], BF16, name="w%d" % c)
+            nc.sync.dma_start(
+                out=w_c[:], in_=weight[r0 : r0 + P * na, :].rearrange("(p a) k -> p a k", a=na)
+            )
+            m_c = const.tile([P, na, K], BF16, name="m%d" % c)
+            nc.sync.dma_start(
+                out=m_c[:], in_=mask[r0 : r0 + P * na, :].rearrange("(p a) k -> p a k", a=na)
+            )
             w_sb.append(w_c)
             m_sb.append(m_c)
         nc.sync.dma_start(out=bias_row[0:1, :], in_=bias.rearrange("(o n) -> o n", o=1))
@@ -81,42 +86,41 @@ def tile_masklockedlinear_t_kernel(tc, x, weight, mask, bias, out):
             x_sb.append(x_c)
 
         mwT = const.tile([P, 4 * N], BF16, name="mwT", align_bytes=64)
-        mwT32 = mwT[:].bitcast(F32).rearrange("q (c p a u) -> q c p a u", c=4, p=P, a=2, u=2)
         junk = const.tile([P, 2, K], BF16, name="junk")
         gram = tp.tile([P, P], F32, name="gram", tag="tp")
-        tot = tp.tile([P, 2], F32, name="tot", tag="tp")
-
-        def stat_mm(i, first, last):
-            nc.tensor.matmul(
-                tot[:], lhsT=ones_f[:], rhs=stats[:, 8 * i : 8 * i + 2], start=first, stop=last
-            )
+        tot = tp.tile([P, 16], F32, name="tot", tag="tp")
 
         mws, pts = [], {}
 
         def mw_transposes(c):
+            na = CHUNKS[c][1]
             mw32 = mws[c][:].rearrange("p t k -> p (t k)").bitcast(F32)
-            pt = accp.tile([P, 2, 2, P], F32, name="pt", tag="acc")
-            for a in range(2):
+            pt = accp.tile([P, na, 2, P], F32, name="pt%d" % na, tag="acc")
+            for a in range(na):
                 for u in range(2):
                     o = 256 * a + P * u
                     nc.tensor.transpose(pt[:, a, u, :], mw32[:, o : o + P], ident[:])
             pts[c] = pt
 
         def mw_exit(c, engine):
+            r0, na = CHUNKS[c]
             src = pts[c][:].rearrange("q a u p -> q p a u")
+            dst = mwT[:, 4 * r0 : 4 * (r0 + P * na)].bitcast(F32)
+            dst = dst.rearrange("q (p a u) -> q p a u", p=P, a=na, u=2)
             if engine == "v":
-                nc.vector.tensor_copy(out=mwT32[:, c], in_=src)
+                nc.vector.tensor_copy(out=dst, in_=src)
             else:
-                nc.scalar.copy(out=mwT32[:, c], in_=src)
+                nc.scalar.copy(out=dst, in_=src)
 
-        for c in range(4):
-            mw_c = const.tile([P, 2, K], BF16, name="mw%d" % c)
+        for c in range(NCH):
+            na = CHUNKS[c][1]
+            mw_c = const.tile([P, na, K], BF16, name="mw%d" % c)
             mws.append(mw_c)
             nc.vector.tensor_tensor(out=mw_c[:], in0=w_sb[c][:], in1=m_sb[c][:], op=ALU.mult)
             nc.scalar.activation(
-                out=junk[:], in_=mw_c[:], func=ACT.Abs, accum_out=stats[:, 8 * c : 8 * c + 1]
+                out=junk[:, 0:na, :], in_=mw_c[:], func=ACT.Abs, accum_out=stats[:, c : c + 1]
             )
-            for a in range(2):
+            for a in range(na):
                 for b in range(4):
                     blk = mw_c[:, a, P * b : P * b + P]
                     nc.tensor.matmul(
@@ -124,25 +128,24 @@ def tile_masklockedlinear_t_kernel(tc, x, weight, mask, bias, out):
                         lhsT=blk,
                         rhs=blk,
                         start=(c == 0 and a == 0 and b == 0),
-                        stop=(c == 3 and a == 1 and b == 3),
+                        stop=(c == NCH - 1 and a == na - 1 and b == 3),
                     )
             if c < 2:
                 mw_transposes(c)
-        for c in range(3):
-            stat_mm(c, c == 0, False)
         mw_exit(0, "v")
         diag = const.tile([P, P], F32, name="diag")
         nc.vector.scalar_tensor_tensor(
             out=diag[:], in0=gram[:], scalar=float(COUNT), in1=ident[:],
-            op0=ALU.mult, op1=ALU.mult, accum_out=stats[:, 33:34],
+            op0=ALU.mult, op1=ALU.mult, accum_out=stats[:, 8:9],
         )
         mw_exit(1, "v")
-        stat_mm(4, False, False)
-        stat_mm(3, False, True)
+        nc.tensor.matmul(tot[:], lhsT=ones_f[:], rhs=stats[:], start=True, stop=True)
 
+        s1 = const.tile([P, 1], F32, name="s1")
+        nc.vector.tensor_reduce(out=s1[:], in_=tot[:, 0:8], axis=AXIS.X, op=ALU.add)
         nv = const.tile([P, 1], F32, name="nv")
-        nc.vector.tensor_scalar(
-            out=nv[:], in0=tot[:, 0:1], scalar1=tot[:, 0:1], scalar2=tot[:, 1:2],
+        nc.vector.scalar_tensor_tensor(
+            out=nv[:], in0=s1[:], scalar=s1[:, 0:1], in1=tot[:, 8:9],
             op0=ALU.mult, op1=ALU.subtract,
         )
         nvc = const.tile([P, 1], F32, name="nvc")
@@ -155,7 +158,7 @@ def tile_masklockedlinear_t_kernel(tc, x, weight, mask, bias, out):
         nc.scalar.mul(out=nthr[:], in_=thr[:], mul=-1.0)
         scl = const.tile([P, 1], F32, name="scl")
         nc.vector.tensor_scalar(
-            out=scl[:], in0=tot[:, 0:1], scalar1=1.0 / COUNT, scalar2=EPS, op0=ALU.mult, op1=ALU.add
+            out=scl[:], in0=s1[:], scalar1=1.0 / COUNT, scalar2=EPS, op0=ALU.mult, op1=ALU.add
         )
 
         xg, xc, xs = {}, [], []
@@ -211,14 +214,14 @@ def tile_masklockedlinear_t_kernel(tc, x, weight, mask, bias, out):
 
         x_bank_t(0, 0)
         x_bank_t(0, 1)
-        mw_transposes(2)
-        mw_transposes(3)
+        for c in range(2, NCH):
+            mw_transposes(c)
         bias_t(0)
         bias_t(1)
         x_bank_s(0, 0)
         x_bank_s(0, 1)
-        mw_exit(2, "s")
-        mw_exit(3, "s")
+        for c in range(2, NCH):
+            mw_exit(c, "s")
         bias_s(0)
 
         tw = const.tile([P, 4 * N], BF16, name="tw", align_bytes=64)

@@ -23,9 +23,7 @@ WT = N // P
 XCH = 4
 TPC = MT // XCH
 GROUPS = [1, 1, 1, 1, 2, 2, 2, 2, 4, 4, 4, 4, 2, 1, 1]
-OB_BUFS = {1: 4, 2: 4, 4: 3}
-CHUNKS = [(0, 2), (256, 2), (512, 2), (768, 1), (896, 1)]
-NCH = len(CHUNKS)
+OB_BUFS = {1: 4, 2: 4, 4: 6}
 EARLY = 3
 
 
@@ -45,263 +43,267 @@ def tile_masklockedlinear_t_kernel(tc, x, weight, mask, bias, out):
         tp = ctx.enter_context(tc.psum_pool(name="tp", bufs=3))
         accp = ctx.enter_context(tc.psum_pool(name="accp", bufs=5))
 
-        bias_row = const.tile([P, N], BF16, name="bias_row")
-        nc.vector.memset(bias_row[:], 0.0)
-        one_col = const.tile([P, 1], F32, name="one_col")
-        nc.vector.memset(one_col[:], 1.0)
-        warm = const.tile([P, 1], F32, name="warm")
-        nc.scalar.activation(out=warm[:], in_=one_col[:], func=ACT.Sqrt)
-        ident = const.tile([P, P], F32, name="ident")
-        make_identity(nc, ident[:])
-        ones_b = const.tile([P, P], BF16, name="ones_b")
-        nc.vector.memset(ones_b[:], 1.0)
-        ones_f = const.tile([P, P], F32, name="ones_f")
-        nc.vector.memset(ones_f[:], 1.0)
-        stats = const.tile([P, 16], F32, name="stats")
-        nc.vector.memset(stats[:], 0.0)
+        pools = {}
+        with tc.tile_pool(name="head", bufs=1) as head:
+            bias_row = head.tile([P, N], BF16, name="bias_row")
+            nc.vector.memset(bias_row[:], 0.0)
+            one_col = const.tile([P, 1], F32, name="one_col")
+            nc.vector.memset(one_col[:], 1.0)
+            warm = const.tile([P, 1], F32, name="warm")
+            nc.scalar.activation(out=warm[:], in_=one_col[:], func=ACT.Sqrt)
+            ident = const.tile([P, P], F32, name="ident")
+            make_identity(nc, ident[:])
+            ones_b = head.tile([P, P], BF16, name="ones_b")
+            nc.vector.memset(ones_b[:], 1.0)
+            ones_f = const.tile([P, P], F32, name="ones_f")
+            nc.vector.memset(ones_f[:], 1.0)
+            stats = const.tile([P, 40], F32, name="stats")
+            nc.vector.memset(stats[:], 0.0)
 
-        x_v = x.rearrange("(p t) k -> p t k", t=MT)
-        out_v = out.rearrange("(p t) n -> p t n", t=MT)
-        w_sb, m_sb = [], []
-        for c in range(NCH):
-            r0, na = CHUNKS[c]
-            w_c = const.tile([P, na, K], BF16, name="w%d" % c)
-            nc.sync.dma_start(
-                out=w_c[:], in_=weight[r0 : r0 + P * na, :].rearrange("(p a) k -> p a k", a=na)
+            w_v = weight.rearrange("(c p a) k -> c p a k", c=4, p=P, a=2)
+            m_v = mask.rearrange("(c p a) k -> c p a k", c=4, p=P, a=2)
+            x_v = x.rearrange("(p t) k -> p t k", t=MT)
+            out_v = out.rearrange("(p t) n -> p t n", t=MT)
+            w_sb, m_sb = [], []
+            for c in range(4):
+                w_c = head.tile([P, 2, K], BF16, name="w%d" % c)
+                nc.sync.dma_start(out=w_c[:], in_=w_v[c])
+                m_c = head.tile([P, 2, K], BF16, name="m%d" % c)
+                nc.sync.dma_start(out=m_c[:], in_=m_v[c])
+                w_sb.append(w_c)
+                m_sb.append(m_c)
+            nc.sync.dma_start(out=bias_row[0:1, :], in_=bias.rearrange("(o n) -> o n", o=1))
+            x_sb = []
+            for j in range(XCH):
+                x_c = const.tile([P, TPC * K], BF16, name="x%d" % j)
+                nc.sync.dma_start(
+                    out=x_c[:].rearrange("p (t k) -> p t k", t=TPC),
+                    in_=x_v[:, TPC * j : TPC * j + TPC, :],
+                )
+                x_sb.append(x_c)
+
+            mwT = head.tile([P, 4 * N], BF16, name="mwT", align_bytes=64)
+            mwT32 = mwT[:].bitcast(F32).rearrange("q (c p a u) -> q c p a u", c=4, p=P, a=2, u=2)
+            junk = head.tile([P, 2, K], BF16, name="junk")
+            gram = tp.tile([P, P], F32, name="gram", tag="tp")
+            tot = tp.tile([P, 2], F32, name="tot", tag="tp")
+
+            def stat_mm(i, first, last):
+                nc.tensor.matmul(
+                    tot[:], lhsT=ones_f[:], rhs=stats[:, 8 * i : 8 * i + 2], start=first, stop=last
+                )
+
+            mws, pts = [], {}
+
+            def mw_transposes(c):
+                mw32 = mws[c][:].rearrange("p t k -> p (t k)").bitcast(F32)
+                pt = accp.tile([P, 2, 2, P], F32, name="pt", tag="acc")
+                for a in range(2):
+                    for u in range(2):
+                        o = 256 * a + P * u
+                        nc.tensor.transpose(pt[:, a, u, :], mw32[:, o : o + P], ident[:])
+                pts[c] = pt
+
+            def mw_exit(c, engine):
+                src = pts[c][:].rearrange("q a u p -> q p a u")
+                if engine == "v":
+                    nc.vector.tensor_copy(out=mwT32[:, c], in_=src)
+                else:
+                    nc.scalar.copy(out=mwT32[:, c], in_=src)
+
+            for c in range(4):
+                mw_c = head.tile([P, 2, K], BF16, name="mw%d" % c)
+                mws.append(mw_c)
+                nc.vector.tensor_tensor(out=mw_c[:], in0=w_sb[c][:], in1=m_sb[c][:], op=ALU.mult)
+                nc.scalar.activation(
+                    out=junk[:], in_=mw_c[:], func=ACT.Abs, accum_out=stats[:, 8 * c : 8 * c + 1]
+                )
+                for a in range(2):
+                    for b in range(4):
+                        blk = mw_c[:, a, P * b : P * b + P]
+                        nc.tensor.matmul(
+                            gram[:],
+                            lhsT=blk,
+                            rhs=blk,
+                            start=(c == 0 and a == 0 and b == 0),
+                            stop=(c == 3 and a == 1 and b == 3),
+                        )
+                if c < 2:
+                    mw_transposes(c)
+            for c in range(3):
+                stat_mm(c, c == 0, False)
+            mw_exit(0, "v")
+            diag = head.tile([P, P], F32, name="diag")
+            nc.vector.scalar_tensor_tensor(
+                out=diag[:], in0=gram[:], scalar=float(COUNT), in1=ident[:],
+                op0=ALU.mult, op1=ALU.mult, accum_out=stats[:, 33:34],
             )
-            m_c = const.tile([P, na, K], BF16, name="m%d" % c)
-            nc.sync.dma_start(
-                out=m_c[:], in_=mask[r0 : r0 + P * na, :].rearrange("(p a) k -> p a k", a=na)
+            mw_exit(1, "v")
+            stat_mm(4, False, False)
+            stat_mm(3, False, True)
+
+            nv = const.tile([P, 1], F32, name="nv")
+            nc.vector.tensor_scalar(
+                out=nv[:], in0=tot[:, 0:1], scalar1=tot[:, 0:1], scalar2=tot[:, 1:2],
+                op0=ALU.mult, op1=ALU.subtract,
             )
-            w_sb.append(w_c)
-            m_sb.append(m_c)
-        nc.sync.dma_start(out=bias_row[0:1, :], in_=bias.rearrange("(o n) -> o n", o=1))
-        x_sb = []
-        for j in range(XCH):
-            x_c = const.tile([P, TPC * K], BF16, name="x%d" % j)
-            nc.sync.dma_start(
-                out=x_c[:].rearrange("p (t k) -> p t k", t=TPC),
-                in_=x_v[:, TPC * j : TPC * j + TPC, :],
-            )
-            x_sb.append(x_c)
-
-        mwT = const.tile([P, 4 * N], BF16, name="mwT", align_bytes=64)
-        junk = const.tile([P, 2, K], BF16, name="junk")
-        gram = tp.tile([P, P], F32, name="gram", tag="tp")
-        tot = tp.tile([P, 16], F32, name="tot", tag="tp")
-
-        mws, pts = [], {}
-
-        def mw_transposes(c):
-            na = CHUNKS[c][1]
-            mw32 = mws[c][:].rearrange("p t k -> p (t k)").bitcast(F32)
-            pt = accp.tile([P, na, 2, P], F32, name="pt%d" % na, tag="acc")
-            for a in range(na):
-                for u in range(2):
-                    o = 256 * a + P * u
-                    nc.tensor.transpose(pt[:, a, u, :], mw32[:, o : o + P], ident[:])
-            pts[c] = pt
-
-        def mw_exit(c, engine):
-            r0, na = CHUNKS[c]
-            src = pts[c][:].rearrange("q a u p -> q p a u")
-            dst = mwT[:, 4 * r0 : 4 * (r0 + P * na)].bitcast(F32)
-            dst = dst.rearrange("q (p a u) -> q p a u", p=P, a=na, u=2)
-            if engine == "v":
-                nc.vector.tensor_copy(out=dst, in_=src)
-            else:
-                nc.scalar.copy(out=dst, in_=src)
-
-        for c in range(NCH):
-            na = CHUNKS[c][1]
-            mw_c = const.tile([P, na, K], BF16, name="mw%d" % c)
-            mws.append(mw_c)
-            nc.vector.tensor_tensor(out=mw_c[:], in0=w_sb[c][:], in1=m_sb[c][:], op=ALU.mult)
+            nvc = const.tile([P, 1], F32, name="nvc")
+            nc.vector.tensor_scalar_min(out=nvc[:], in0=nv[:], scalar1=0.0)
+            thr = const.tile([P, 1], F32, name="thr")
             nc.scalar.activation(
-                out=junk[:, 0:na, :], in_=mw_c[:], func=ACT.Abs, accum_out=stats[:, c : c + 1]
+                out=thr[:], in_=nvc[:], func=ACT.Sqrt, scale=-1.0 / (4.0 * COUNT * (COUNT - 1.0))
             )
-            for a in range(na):
-                for b in range(4):
-                    blk = mw_c[:, a, P * b : P * b + P]
-                    nc.tensor.matmul(
-                        gram[:],
-                        lhsT=blk,
-                        rhs=blk,
-                        start=(c == 0 and a == 0 and b == 0),
-                        stop=(c == NCH - 1 and a == na - 1 and b == 3),
-                    )
-            if c < 2:
-                mw_transposes(c)
-        mw_exit(0, "v")
-        diag = const.tile([P, P], F32, name="diag")
-        nc.vector.scalar_tensor_tensor(
-            out=diag[:], in0=gram[:], scalar=float(COUNT), in1=ident[:],
-            op0=ALU.mult, op1=ALU.mult, accum_out=stats[:, 8:9],
-        )
-        mw_exit(1, "v")
-        nc.tensor.matmul(tot[:], lhsT=ones_f[:], rhs=stats[:], start=True, stop=True)
-
-        s1 = const.tile([P, 1], F32, name="s1")
-        nc.vector.tensor_reduce(out=s1[:], in_=tot[:, 0:8], axis=AXIS.X, op=ALU.add)
-        nv = const.tile([P, 1], F32, name="nv")
-        nc.vector.scalar_tensor_tensor(
-            out=nv[:], in0=s1[:], scalar=s1[:, 0:1], in1=tot[:, 8:9],
-            op0=ALU.mult, op1=ALU.subtract,
-        )
-        nvc = const.tile([P, 1], F32, name="nvc")
-        nc.vector.tensor_scalar_min(out=nvc[:], in0=nv[:], scalar1=0.0)
-        thr = const.tile([P, 1], F32, name="thr")
-        nc.scalar.activation(
-            out=thr[:], in_=nvc[:], func=ACT.Sqrt, scale=-1.0 / (4.0 * COUNT * (COUNT - 1.0))
-        )
-        nthr = const.tile([P, 1], F32, name="nthr")
-        nc.scalar.mul(out=nthr[:], in_=thr[:], mul=-1.0)
-        scl = const.tile([P, 1], F32, name="scl")
-        nc.vector.tensor_scalar(
-            out=scl[:], in0=s1[:], scalar1=1.0 / COUNT, scalar2=EPS, op0=ALU.mult, op1=ALU.add
-        )
-
-        xg, xc, xs = {}, [], []
-        for j in range(XCH):
-            xc.append(const.tile([P, TPC * P], U32, name="xc%d" % j, align_bytes=64))
-            xs.append(const.tile([P, TPC * P], U8, name="xs%d" % j, align_bytes=64))
-
-        xts = {}
-
-        def x_bank_t(j, b):
-            x32 = x_sb[j][:].bitcast(F32)
-            xt = tp.tile([P, 2, 2, P], F32, name="xt", tag="tp")
-            for a in range(2):
-                for u in range(2):
-                    o = 256 * (2 * b + a) + P * u
-                    nc.tensor.transpose(xt[:, a, u, :], x32[:, o : o + P], ident[:])
-            xts[(j, b)] = xt
-
-        def x_bank_s(j, b):
-            xt = xts[(j, b)]
-            if j not in xg:
-                xg[j] = xgp.tile([P, TPC * K], BF16, name="xg", tag="xg", align_bytes=64)
-            dst = xg[j][:].bitcast(F32)[:, 512 * b : 512 * b + 512]
-            nc.scalar.copy(
-                out=dst.rearrange("q (a p u) -> q a p u", a=2, p=P, u=2),
-                in_=xt[:].rearrange("q a u p -> q a p u"),
-            )
-
-        def x_quant(j, b0, nb):
-            nc.vector.quantize_mx(
-                out=xc[j][:, 256 * b0 : 256 * (b0 + nb)].bitcast(FP8X4),
-                scales=xs[j][:, 256 * b0 : 256 * (b0 + nb)],
-                in_=xg[j][:, 1024 * b0 : 1024 * (b0 + nb)],
-            )
-
-        def x_pair(i):
-            for b in (2 * (i % 2), 2 * (i % 2) + 1):
-                x_bank_t(1 + i // 2, b)
-                x_bank_s(1 + i // 2, b)
-
-        bias_sb = const.tile([P, N], F32, name="bias_sb")
-        pbs = {}
-
-        def bias_t(h):
-            pb = accp.tile([P, 512], F32, name="pb", tag="acc")
-            nc.tensor.matmul(
-                pb[:], lhsT=ones_b[:], rhs=bias_row[:, 512 * h : 512 * h + 512], start=True, stop=True
-            )
-            pbs[h] = pb
-
-        def bias_s(h):
-            nc.scalar.copy(out=bias_sb[:, 512 * h : 512 * h + 512], in_=pbs[h][:])
-
-        x_bank_t(0, 0)
-        x_bank_t(0, 1)
-        for c in range(2, NCH):
-            mw_transposes(c)
-        bias_t(0)
-        bias_t(1)
-        x_bank_s(0, 0)
-        x_bank_s(0, 1)
-        for c in range(2, NCH):
-            mw_exit(c, "s")
-        bias_s(0)
-
-        tw = const.tile([P, 4 * N], BF16, name="tw", align_bytes=64)
-        neg = const.tile([P, 2 * N], BF16, name="neg")
-        twc = const.tile([P, N], U32, name="twc", align_bytes=64)
-        tws = const.tile([P, N], U8, name="tws", align_bytes=64)
-
-        def tern(h):
-            cols = slice(2048 * h, 2048 * h + 2048)
+            nthr = const.tile([P, 1], F32, name="nthr")
+            nc.scalar.mul(out=nthr[:], in_=thr[:], mul=-1.0)
+            scl = const.tile([P, 1], F32, name="scl")
             nc.vector.tensor_scalar(
-                out=tw[:, cols], in0=mwT[:, cols], scalar1=thr[:, 0:1], scalar2=scl[:, 0:1],
-                op0=ALU.is_gt, op1=ALU.mult,
-            )
-            nc.vector.tensor_scalar(
-                out=neg[:], in0=mwT[:, cols], scalar1=nthr[:, 0:1], scalar2=scl[:, 0:1],
-                op0=ALU.is_lt, op1=ALU.mult,
-            )
-            nc.vector.tensor_tensor(
-                out=tw[:, cols], in0=tw[:, cols], in1=neg[:], op=ALU.subtract
+                out=scl[:], in0=tot[:, 0:1], scalar1=1.0 / COUNT, scalar2=EPS, op0=ALU.mult, op1=ALU.add
             )
 
-        def tw_quant(h):
-            nc.vector.quantize_mx(
-                out=twc[:, 512 * h : 512 * h + 512].bitcast(FP8X4),
-                scales=tws[:, 512 * h : 512 * h + 512],
-                in_=tw[:, 2048 * h : 2048 * h + 2048],
-            )
+            xg, xc, xs = {}, [], []
+            for j in range(XCH):
+                xc.append(const.tile([P, TPC * P], U32, name="xc%d" % j, align_bytes=64))
+                xs.append(const.tile([P, TPC * P], U8, name="xs%d" % j, align_bytes=64))
 
-        obs = {}
-        first_of = {}
-        size_of = {}
-        t0 = 0
-        for g in GROUPS:
-            for i in range(g):
-                first_of[t0 + i] = t0
-            size_of[t0] = g
-            t0 += g
+            xts = {}
 
-        def unit(t, h):
-            f = first_of[t]
-            if f not in obs:
-                g = size_of[f]
-                obs[f] = outp.tile([P, g, N], F32, name="ob%d" % g, tag="ob%d" % g, bufs=OB_BUFS[g])
-            ob = obs[f]
-            i = t - f
-            j, tl = divmod(t, TPC)
-            cols = slice(512 * h, 512 * h + 512)
-            acc = accp.tile([P, 512], F32, name="acc", tag="acc")
-            nc.tensor.matmul_mx(
-                out=acc[:],
-                lhsT=xc[j][:, P * tl : P * tl + P].bitcast(FP8X4),
-                lhsT_scale=xs[j][:, P * tl : P * tl + P],
-                rhs=twc[:, cols].bitcast(FP8X4),
-                rhs_scale=tws[:, cols],
-                start=True,
-                stop=True,
-            )
-            if on_scalar_and_gpsimd(t, h):
-                nc.scalar.copy(out=ob[:, i, cols], in_=acc[:])
-                nc.gpsimd.tensor_tensor(
-                    out=ob[:, i, cols], in0=ob[:, i, cols], in1=bias_sb[:, cols], op=ALU.add
+            def x_bank_t(j, b):
+                x32 = x_sb[j][:].bitcast(F32)
+                xt = tp.tile([P, 2, 2, P], F32, name="xt", tag="tp")
+                for a in range(2):
+                    for u in range(2):
+                        o = 256 * (2 * b + a) + P * u
+                        nc.tensor.transpose(xt[:, a, u, :], x32[:, o : o + P], ident[:])
+                xts[(j, b)] = xt
+
+            def x_bank_s(j, b):
+                xt = xts[(j, b)]
+                if j not in xg:
+                    xg[j] = xgp.tile([P, TPC * K], BF16, name="xg", tag="xg", align_bytes=64)
+                dst = xg[j][:].bitcast(F32)[:, 512 * b : 512 * b + 512]
+                nc.scalar.copy(
+                    out=dst.rearrange("q (a p u) -> q a p u", a=2, p=P, u=2),
+                    in_=xt[:].rearrange("q a u p -> q a p u"),
                 )
-            else:
+
+            def x_quant(j, b0, nb):
+                nc.vector.quantize_mx(
+                    out=xc[j][:, 256 * b0 : 256 * (b0 + nb)].bitcast(FP8X4),
+                    scales=xs[j][:, 256 * b0 : 256 * (b0 + nb)],
+                    in_=xg[j][:, 1024 * b0 : 1024 * (b0 + nb)],
+                )
+
+            def x_pair(i):
+                for b in (2 * (i % 2), 2 * (i % 2) + 1):
+                    x_bank_t(1 + i // 2, b)
+                    x_bank_s(1 + i // 2, b)
+
+            bias_sb = const.tile([P, N], F32, name="bias_sb")
+            pbs = {}
+
+            def bias_t(h):
+                pb = accp.tile([P, 512], F32, name="pb", tag="acc")
+                nc.tensor.matmul(
+                    pb[:], lhsT=ones_b[:], rhs=bias_row[:, 512 * h : 512 * h + 512], start=True, stop=True
+                )
+                pbs[h] = pb
+
+            def bias_s(h):
+                nc.scalar.copy(out=bias_sb[:, 512 * h : 512 * h + 512], in_=pbs[h][:])
+
+            x_bank_t(0, 0)
+            x_bank_t(0, 1)
+            mw_transposes(2)
+            mw_transposes(3)
+            bias_t(0)
+            bias_t(1)
+            x_bank_s(0, 0)
+            x_bank_s(0, 1)
+            mw_exit(2, "s")
+            mw_exit(3, "s")
+            bias_s(0)
+
+            tw = head.tile([P, 4 * N], BF16, name="tw", align_bytes=64)
+            neg = head.tile([P, 2 * N], BF16, name="neg")
+            twc = const.tile([P, N], U32, name="twc", align_bytes=64)
+            tws = const.tile([P, N], U8, name="tws", align_bytes=64)
+
+            def tern(h):
+                cols = slice(2048 * h, 2048 * h + 2048)
+                nc.vector.tensor_scalar(
+                    out=tw[:, cols], in0=mwT[:, cols], scalar1=thr[:, 0:1], scalar2=scl[:, 0:1],
+                    op0=ALU.is_gt, op1=ALU.mult,
+                )
+                nc.vector.tensor_scalar(
+                    out=neg[:], in0=mwT[:, cols], scalar1=nthr[:, 0:1], scalar2=scl[:, 0:1],
+                    op0=ALU.is_lt, op1=ALU.mult,
+                )
                 nc.vector.tensor_tensor(
-                    out=ob[:, i, cols], in0=acc[:], in1=bias_sb[:, cols], op=ALU.add
+                    out=tw[:, cols], in0=tw[:, cols], in1=neg[:], op=ALU.subtract
                 )
 
-        tern(0)
-        x_quant(0, 0, 1)
-        tw_quant(0)
-        x_quant(0, 1, 1)
-        unit(0, 0)
-        bias_s(1)
-        for t in range(1, EARLY):
-            unit(t, 0)
-        for b in (2, 3):
-            x_bank_t(0, b)
-            x_bank_s(0, b)
-        tern(1)
-        tw_quant(1)
+            def tw_quant(h):
+                nc.vector.quantize_mx(
+                    out=twc[:, 512 * h : 512 * h + 512].bitcast(FP8X4),
+                    scales=tws[:, 512 * h : 512 * h + 512],
+                    in_=tw[:, 2048 * h : 2048 * h + 2048],
+                )
+
+            obs = {}
+            first_of = {}
+            size_of = {}
+            t0 = 0
+            for g in GROUPS:
+                for i in range(g):
+                    first_of[t0 + i] = t0
+                size_of[t0] = g
+                t0 += g
+
+            def unit(t, h):
+                f = first_of[t]
+                if f not in obs:
+                    g = size_of[f]
+                    obs[f] = pools.get(g, outp).tile(
+                        [P, g, N], F32, name="ob%d" % g, tag="ob%d" % g, bufs=OB_BUFS[g]
+                    )
+                ob = obs[f]
+                i = t - f
+                j, tl = divmod(t, TPC)
+                cols = slice(512 * h, 512 * h + 512)
+                acc = accp.tile([P, 512], F32, name="acc", tag="acc")
+                nc.tensor.matmul_mx(
+                    out=acc[:],
+                    lhsT=xc[j][:, P * tl : P * tl + P].bitcast(FP8X4),
+                    lhsT_scale=xs[j][:, P * tl : P * tl + P],
+                    rhs=twc[:, cols].bitcast(FP8X4),
+                    rhs_scale=tws[:, cols],
+                    start=True,
+                    stop=True,
+                )
+                if on_scalar_and_gpsimd(t, h):
+                    nc.scalar.copy(out=ob[:, i, cols], in_=acc[:])
+                    nc.gpsimd.tensor_tensor(
+                        out=ob[:, i, cols], in0=ob[:, i, cols], in1=bias_sb[:, cols], op=ALU.add
+                    )
+                else:
+                    nc.vector.tensor_tensor(
+                        out=ob[:, i, cols], in0=acc[:], in1=bias_sb[:, cols], op=ALU.add
+                    )
+
+            tern(0)
+            x_quant(0, 0, 1)
+            tw_quant(0)
+            x_quant(0, 1, 1)
+            unit(0, 0)
+            bias_s(1)
+            for t in range(1, EARLY):
+                unit(t, 0)
+            for b in (2, 3):
+                x_bank_t(0, b)
+                x_bank_s(0, b)
+            tern(1)
+            tw_quant(1)
+        pools[4] = ctx.enter_context(tc.tile_pool(name="big", bufs=1))
 
         for t in range(MT):
             if t >= EARLY:

@@ -23,7 +23,7 @@ WT = N // P
 XCH = 4
 TPC = MT // XCH
 GROUPS = [1, 1, 1, 1, 2, 2, 2, 2, 4, 4, 4, 4, 2, 1, 1]
-OB_BUFS = {1: 4, 2: 4, 4: 6}
+OB_BUFS = {1: 4, 2: 4, 4: 3}
 EARLY = 3
 
 
@@ -36,274 +36,268 @@ def on_scalar_and_gpsimd(t, h):
 def tile_masklockedlinear_t_kernel(tc, x, weight, mask, bias, out):
     nc = tc.nc
     with ExitStack() as ctx:
-        ctx.enter_context(tc.manual_schedule())
         const = ctx.enter_context(tc.tile_pool(name="const", bufs=1))
         outp = ctx.enter_context(tc.tile_pool(name="outp", bufs=1))
         xgp = ctx.enter_context(tc.tile_pool(name="xgp", bufs=2))
         tp = ctx.enter_context(tc.psum_pool(name="tp", bufs=3))
         accp = ctx.enter_context(tc.psum_pool(name="accp", bufs=5))
 
-        pools = {}
-        with tc.tile_pool(name="head", bufs=1) as head:
-            bias_row = head.tile([P, N], BF16, name="bias_row")
-            nc.vector.memset(bias_row[:], 0.0)
-            one_col = const.tile([P, 1], F32, name="one_col")
-            nc.vector.memset(one_col[:], 1.0)
-            warm = const.tile([P, 1], F32, name="warm")
-            nc.scalar.activation(out=warm[:], in_=one_col[:], func=ACT.Sqrt)
-            ident = const.tile([P, P], F32, name="ident")
-            make_identity(nc, ident[:])
-            ones_b = head.tile([P, P], BF16, name="ones_b")
-            nc.vector.memset(ones_b[:], 1.0)
-            ones_f = const.tile([P, P], F32, name="ones_f")
-            nc.vector.memset(ones_f[:], 1.0)
-            stats = const.tile([P, 40], F32, name="stats")
-            nc.vector.memset(stats[:], 0.0)
+        bias_row = const.tile([P, N], BF16, name="bias_row")
+        nc.vector.memset(bias_row[:], 0.0)
+        one_col = const.tile([P, 1], F32, name="one_col")
+        nc.vector.memset(one_col[:], 1.0)
+        warm = const.tile([P, 1], F32, name="warm")
+        nc.scalar.activation(out=warm[:], in_=one_col[:], func=ACT.Sqrt)
+        ident = const.tile([P, P], F32, name="ident")
+        make_identity(nc, ident[:])
+        ones_b = const.tile([P, P], BF16, name="ones_b")
+        nc.vector.memset(ones_b[:], 1.0)
+        ones_f = const.tile([P, P], F32, name="ones_f")
+        nc.vector.memset(ones_f[:], 1.0)
+        stats = const.tile([P, 40], F32, name="stats")
+        nc.vector.memset(stats[:], 0.0)
 
-            w_v = weight.rearrange("(c p a) k -> c p a k", c=4, p=P, a=2)
-            m_v = mask.rearrange("(c p a) k -> c p a k", c=4, p=P, a=2)
-            x_v = x.rearrange("(p t) k -> p t k", t=MT)
-            out_v = out.rearrange("(p t) n -> p t n", t=MT)
-            w_sb, m_sb = [], []
-            for c in range(4):
-                w_c = head.tile([P, 2, K], BF16, name="w%d" % c)
-                nc.sync.dma_start(out=w_c[:], in_=w_v[c])
-                m_c = head.tile([P, 2, K], BF16, name="m%d" % c)
-                nc.sync.dma_start(out=m_c[:], in_=m_v[c])
-                w_sb.append(w_c)
-                m_sb.append(m_c)
-            nc.sync.dma_start(out=bias_row[0:1, :], in_=bias.rearrange("(o n) -> o n", o=1))
-            x_sb = []
-            for j in range(XCH):
-                x_c = const.tile([P, TPC * K], BF16, name="x%d" % j)
-                nc.sync.dma_start(
-                    out=x_c[:].rearrange("p (t k) -> p t k", t=TPC),
-                    in_=x_v[:, TPC * j : TPC * j + TPC, :],
-                )
-                x_sb.append(x_c)
-
-            mwT = head.tile([P, 4 * N], BF16, name="mwT", align_bytes=64)
-            mwT32 = mwT[:].bitcast(F32).rearrange("q (c p a u) -> q c p a u", c=4, p=P, a=2, u=2)
-            junk = head.tile([P, 2, K], BF16, name="junk")
-            gram = tp.tile([P, P], F32, name="gram", tag="tp")
-            tot = tp.tile([P, 2], F32, name="tot", tag="tp")
-
-            def stat_mm(i, first, last):
-                nc.tensor.matmul(
-                    tot[:], lhsT=ones_f[:], rhs=stats[:, 8 * i : 8 * i + 2], start=first, stop=last
-                )
-
-            mws, pts = [], {}
-
-            def mw_transposes(c):
-                mw32 = mws[c][:].rearrange("p t k -> p (t k)").bitcast(F32)
-                pt = accp.tile([P, 2, 2, P], F32, name="pt", tag="acc")
-                for a in range(2):
-                    for u in range(2):
-                        o = 256 * a + P * u
-                        nc.tensor.transpose(pt[:, a, u, :], mw32[:, o : o + P], ident[:])
-                pts[c] = pt
-
-            def mw_exit(c, engine):
-                src = pts[c][:].rearrange("q a u p -> q p a u")
-                if engine == "v":
-                    nc.vector.tensor_copy(out=mwT32[:, c], in_=src)
-                else:
-                    nc.scalar.copy(out=mwT32[:, c], in_=src)
-
-            for c in range(4):
-                mw_c = head.tile([P, 2, K], BF16, name="mw%d" % c)
-                mws.append(mw_c)
-                nc.vector.tensor_tensor(out=mw_c[:], in0=w_sb[c][:], in1=m_sb[c][:], op=ALU.mult)
-                nc.scalar.activation(
-                    out=junk[:], in_=mw_c[:], func=ACT.Abs, accum_out=stats[:, 8 * c : 8 * c + 1]
-                )
-                for a in range(2):
-                    for b in range(4):
-                        blk = mw_c[:, a, P * b : P * b + P]
-                        nc.tensor.matmul(
-                            gram[:],
-                            lhsT=blk,
-                            rhs=blk,
-                            start=(c == 0 and a == 0 and b == 0),
-                            stop=(c == 3 and a == 1 and b == 3),
-                        )
-                if c < 2:
-                    mw_transposes(c)
-            for c in range(3):
-                stat_mm(c, c == 0, False)
-            mw_exit(0, "v")
-            diag = head.tile([P, P], F32, name="diag")
-            nc.vector.scalar_tensor_tensor(
-                out=diag[:], in0=gram[:], scalar=float(COUNT), in1=ident[:],
-                op0=ALU.mult, op1=ALU.mult, accum_out=stats[:, 33:34],
+        w_v = weight.rearrange("(c p a) k -> c p a k", c=4, p=P, a=2)
+        m_v = mask.rearrange("(c p a) k -> c p a k", c=4, p=P, a=2)
+        x_v = x.rearrange("(p t) k -> p t k", t=MT)
+        out_v = out.rearrange("(p t) n -> p t n", t=MT)
+        w_sb, m_sb = [], []
+        for c in range(4):
+            w_c = const.tile([P, 2, K], BF16, name="w%d" % c)
+            nc.sync.dma_start(out=w_c[:], in_=w_v[c])
+            m_c = const.tile([P, 2, K], BF16, name="m%d" % c)
+            nc.sync.dma_start(out=m_c[:], in_=m_v[c])
+            w_sb.append(w_c)
+            m_sb.append(m_c)
+        nc.sync.dma_start(out=bias_row[0:1, :], in_=bias.rearrange("(o n) -> o n", o=1))
+        x_sb = []
+        for j in range(XCH):
+            x_c = const.tile([P, TPC * K], BF16, name="x%d" % j)
+            nc.sync.dma_start(
+                out=x_c[:].rearrange("p (t k) -> p t k", t=TPC),
+                in_=x_v[:, TPC * j : TPC * j + TPC, :],
             )
-            mw_exit(1, "v")
-            stat_mm(4, False, False)
-            stat_mm(3, False, True)
+            x_sb.append(x_c)
 
-            nv = const.tile([P, 1], F32, name="nv")
-            nc.vector.tensor_scalar(
-                out=nv[:], in0=tot[:, 0:1], scalar1=tot[:, 0:1], scalar2=tot[:, 1:2],
-                op0=ALU.mult, op1=ALU.subtract,
+        mwT = const.tile([P, 4 * N], BF16, name="mwT", align_bytes=64)
+        mwT32 = mwT[:].bitcast(F32).rearrange("q (c p a u) -> q c p a u", c=4, p=P, a=2, u=2)
+        junk = const.tile([P, 2, K], BF16, name="junk")
+        gram = tp.tile([P, P], F32, name="gram", tag="tp")
+        tot = tp.tile([P, 2], F32, name="tot", tag="tp")
+
+        def stat_mm(i, first, last):
+            nc.tensor.matmul(
+                tot[:], lhsT=ones_f[:], rhs=stats[:, 8 * i : 8 * i + 2], start=first, stop=last
             )
-            nvc = const.tile([P, 1], F32, name="nvc")
-            nc.vector.tensor_scalar_min(out=nvc[:], in0=nv[:], scalar1=0.0)
-            thr = const.tile([P, 1], F32, name="thr")
+
+        mws, pts = [], {}
+
+        def mw_transposes(c):
+            mw32 = mws[c][:].rearrange("p t k -> p (t k)").bitcast(F32)
+            pt = accp.tile([P, 2, 2, P], F32, name="pt", tag="acc")
+            for a in range(2):
+                for u in range(2):
+                    o = 256 * a + P * u
+                    nc.tensor.transpose(pt[:, a, u, :], mw32[:, o : o + P], ident[:])
+            pts[c] = pt
+
+        def mw_exit(c, engine):
+            src = pts[c][:].rearrange("q a u p -> q p a u")
+            if engine == "v":
+                nc.vector.tensor_copy(out=mwT32[:, c], in_=src)
+            else:
+                nc.scalar.copy(out=mwT32[:, c], in_=src)
+
+        for c in range(4):
+            mw_c = const.tile([P, 2, K], BF16, name="mw%d" % c)
+            mws.append(mw_c)
+            nc.vector.tensor_tensor(out=mw_c[:], in0=w_sb[c][:], in1=m_sb[c][:], op=ALU.mult)
             nc.scalar.activation(
-                out=thr[:], in_=nvc[:], func=ACT.Sqrt, scale=-1.0 / (4.0 * COUNT * (COUNT - 1.0))
+                out=junk[:], in_=mw_c[:], func=ACT.Abs, accum_out=stats[:, 8 * c : 8 * c + 1]
             )
-            nthr = const.tile([P, 1], F32, name="nthr")
-            nc.scalar.mul(out=nthr[:], in_=thr[:], mul=-1.0)
-            scl = const.tile([P, 1], F32, name="scl")
+            for a in range(2):
+                for b in range(4):
+                    blk = mw_c[:, a, P * b : P * b + P]
+                    nc.tensor.matmul(
+                        gram[:],
+                        lhsT=blk,
+                        rhs=blk,
+                        start=(c == 0 and a == 0 and b == 0),
+                        stop=(c == 3 and a == 1 and b == 3),
+                    )
+            if c < 2:
+                mw_transposes(c)
+        for c in range(3):
+            stat_mm(c, c == 0, False)
+        mw_exit(0, "v")
+        diag = const.tile([P, P], F32, name="diag")
+        nc.vector.scalar_tensor_tensor(
+            out=diag[:], in0=gram[:], scalar=float(COUNT), in1=ident[:],
+            op0=ALU.mult, op1=ALU.mult, accum_out=stats[:, 33:34],
+        )
+        mw_exit(1, "v")
+        stat_mm(4, False, False)
+        stat_mm(3, False, True)
+
+        nv = const.tile([P, 1], F32, name="nv")
+        nc.vector.tensor_scalar(
+            out=nv[:], in0=tot[:, 0:1], scalar1=tot[:, 0:1], scalar2=tot[:, 1:2],
+            op0=ALU.mult, op1=ALU.subtract,
+        )
+        nvc = const.tile([P, 1], F32, name="nvc")
+        nc.vector.tensor_scalar_min(out=nvc[:], in0=nv[:], scalar1=0.0)
+        thr = const.tile([P, 1], F32, name="thr")
+        nc.scalar.activation(
+            out=thr[:], in_=nvc[:], func=ACT.Sqrt, scale=-1.0 / (4.0 * COUNT * (COUNT - 1.0))
+        )
+        nthr = const.tile([P, 1], F32, name="nthr")
+        nc.scalar.mul(out=nthr[:], in_=thr[:], mul=-1.0)
+        scl = const.tile([P, 1], F32, name="scl")
+        nc.vector.tensor_scalar(
+            out=scl[:], in0=tot[:, 0:1], scalar1=1.0 / COUNT, scalar2=EPS, op0=ALU.mult, op1=ALU.add
+        )
+
+        xg, xc, xs = {}, [], []
+        for j in range(XCH):
+            xc.append(const.tile([P, TPC * P], U32, name="xc%d" % j, align_bytes=64))
+            xs.append(const.tile([P, TPC * P], U8, name="xs%d" % j, align_bytes=64))
+
+        xts = {}
+
+        def x_bank_t(j, b):
+            x32 = x_sb[j][:].bitcast(F32)
+            xt = tp.tile([P, 2, 2, P], F32, name="xt", tag="tp")
+            for a in range(2):
+                for u in range(2):
+                    o = 256 * (2 * b + a) + P * u
+                    nc.tensor.transpose(xt[:, a, u, :], x32[:, o : o + P], ident[:])
+            xts[(j, b)] = xt
+
+        def x_bank_s(j, b):
+            xt = xts[(j, b)]
+            if j not in xg:
+                xg[j] = xgp.tile([P, TPC * K], BF16, name="xg", tag="xg", align_bytes=64)
+            dst = xg[j][:].bitcast(F32)[:, 512 * b : 512 * b + 512]
+            nc.scalar.copy(
+                out=dst.rearrange("q (a p u) -> q a p u", a=2, p=P, u=2),
+                in_=xt[:].rearrange("q a u p -> q a p u"),
+            )
+
+        def x_quant(j, b0, nb):
+            nc.vector.quantize_mx(
+                out=xc[j][:, 256 * b0 : 256 * (b0 + nb)].bitcast(FP8X4),
+                scales=xs[j][:, 256 * b0 : 256 * (b0 + nb)],
+                in_=xg[j][:, 1024 * b0 : 1024 * (b0 + nb)],
+            )
+
+        def x_pair(i):
+            for b in (2 * (i % 2), 2 * (i % 2) + 1):
+                x_bank_t(1 + i // 2, b)
+                x_bank_s(1 + i // 2, b)
+
+        bias_sb = const.tile([P, N], F32, name="bias_sb")
+        pbs = {}
+
+        def bias_t(h):
+            pb = accp.tile([P, 512], F32, name="pb", tag="acc")
+            nc.tensor.matmul(
+                pb[:], lhsT=ones_b[:], rhs=bias_row[:, 512 * h : 512 * h + 512], start=True, stop=True
+            )
+            pbs[h] = pb
+
+        def bias_s(h):
+            nc.scalar.copy(out=bias_sb[:, 512 * h : 512 * h + 512], in_=pbs[h][:])
+
+        x_bank_t(0, 0)
+        x_bank_t(0, 1)
+        mw_transposes(2)
+        mw_transposes(3)
+        bias_t(0)
+        bias_t(1)
+        x_bank_s(0, 0)
+        x_bank_s(0, 1)
+        mw_exit(2, "s")
+        mw_exit(3, "s")
+        bias_s(0)
+
+        tw = const.tile([P, 4 * N], BF16, name="tw", align_bytes=64)
+        neg = const.tile([P, 2 * N], BF16, name="neg")
+        twc = const.tile([P, N], U32, name="twc", align_bytes=64)
+        tws = const.tile([P, N], U8, name="tws", align_bytes=64)
+
+        def tern(h):
+            cols = slice(2048 * h, 2048 * h + 2048)
             nc.vector.tensor_scalar(
-                out=scl[:], in0=tot[:, 0:1], scalar1=1.0 / COUNT, scalar2=EPS, op0=ALU.mult, op1=ALU.add
+                out=tw[:, cols], in0=mwT[:, cols], scalar1=thr[:, 0:1], scalar2=scl[:, 0:1],
+                op0=ALU.is_gt, op1=ALU.mult,
+            )
+            nc.vector.tensor_scalar(
+                out=neg[:], in0=mwT[:, cols], scalar1=nthr[:, 0:1], scalar2=scl[:, 0:1],
+                op0=ALU.is_lt, op1=ALU.mult,
+            )
+            nc.vector.tensor_tensor(
+                out=tw[:, cols], in0=tw[:, cols], in1=neg[:], op=ALU.subtract
             )
 
-            xg, xc, xs = {}, [], []
-            for j in range(XCH):
-                xc.append(const.tile([P, TPC * P], U32, name="xc%d" % j, align_bytes=64))
-                xs.append(const.tile([P, TPC * P], U8, name="xs%d" % j, align_bytes=64))
+        def tw_quant(h):
+            nc.vector.quantize_mx(
+                out=twc[:, 512 * h : 512 * h + 512].bitcast(FP8X4),
+                scales=tws[:, 512 * h : 512 * h + 512],
+                in_=tw[:, 2048 * h : 2048 * h + 2048],
+            )
 
-            xts = {}
+        obs = {}
+        first_of = {}
+        size_of = {}
+        t0 = 0
+        for g in GROUPS:
+            for i in range(g):
+                first_of[t0 + i] = t0
+            size_of[t0] = g
+            t0 += g
 
-            def x_bank_t(j, b):
-                x32 = x_sb[j][:].bitcast(F32)
-                xt = tp.tile([P, 2, 2, P], F32, name="xt", tag="tp")
-                for a in range(2):
-                    for u in range(2):
-                        o = 256 * (2 * b + a) + P * u
-                        nc.tensor.transpose(xt[:, a, u, :], x32[:, o : o + P], ident[:])
-                xts[(j, b)] = xt
-
-            def x_bank_s(j, b):
-                xt = xts[(j, b)]
-                if j not in xg:
-                    xg[j] = xgp.tile([P, TPC * K], BF16, name="xg", tag="xg", align_bytes=64)
-                dst = xg[j][:].bitcast(F32)[:, 512 * b : 512 * b + 512]
-                nc.scalar.copy(
-                    out=dst.rearrange("q (a p u) -> q a p u", a=2, p=P, u=2),
-                    in_=xt[:].rearrange("q a u p -> q a p u"),
+        def unit(t, h):
+            f = first_of[t]
+            if f not in obs:
+                g = size_of[f]
+                obs[f] = outp.tile([P, g, N], F32, name="ob%d" % g, tag="ob%d" % g, bufs=OB_BUFS[g])
+            ob = obs[f]
+            i = t - f
+            j, tl = divmod(t, TPC)
+            cols = slice(512 * h, 512 * h + 512)
+            acc = accp.tile([P, 512], F32, name="acc", tag="acc")
+            nc.tensor.matmul_mx(
+                out=acc[:],
+                lhsT=xc[j][:, P * tl : P * tl + P].bitcast(FP8X4),
+                lhsT_scale=xs[j][:, P * tl : P * tl + P],
+                rhs=twc[:, cols].bitcast(FP8X4),
+                rhs_scale=tws[:, cols],
+                start=True,
+                stop=True,
+            )
+            if on_scalar_and_gpsimd(t, h):
+                nc.scalar.copy(out=ob[:, i, cols], in_=acc[:])
+                nc.gpsimd.tensor_tensor(
+                    out=ob[:, i, cols], in0=ob[:, i, cols], in1=bias_sb[:, cols], op=ALU.add
                 )
-
-            def x_quant(j, b0, nb):
-                nc.vector.quantize_mx(
-                    out=xc[j][:, 256 * b0 : 256 * (b0 + nb)].bitcast(FP8X4),
-                    scales=xs[j][:, 256 * b0 : 256 * (b0 + nb)],
-                    in_=xg[j][:, 1024 * b0 : 1024 * (b0 + nb)],
-                )
-
-            def x_pair(i):
-                for b in (2 * (i % 2), 2 * (i % 2) + 1):
-                    x_bank_t(1 + i // 2, b)
-                    x_bank_s(1 + i // 2, b)
-
-            bias_sb = const.tile([P, N], F32, name="bias_sb")
-            pbs = {}
-
-            def bias_t(h):
-                pb = accp.tile([P, 512], F32, name="pb", tag="acc")
-                nc.tensor.matmul(
-                    pb[:], lhsT=ones_b[:], rhs=bias_row[:, 512 * h : 512 * h + 512], start=True, stop=True
-                )
-                pbs[h] = pb
-
-            def bias_s(h):
-                nc.scalar.copy(out=bias_sb[:, 512 * h : 512 * h + 512], in_=pbs[h][:])
-
-            x_bank_t(0, 0)
-            x_bank_t(0, 1)
-            mw_transposes(2)
-            mw_transposes(3)
-            bias_t(0)
-            bias_t(1)
-            x_bank_s(0, 0)
-            x_bank_s(0, 1)
-            mw_exit(2, "s")
-            mw_exit(3, "s")
-            bias_s(0)
-
-            tw = head.tile([P, 4 * N], BF16, name="tw", align_bytes=64)
-            neg = head.tile([P, 2 * N], BF16, name="neg")
-            twc = const.tile([P, N], U32, name="twc", align_bytes=64)
-            tws = const.tile([P, N], U8, name="tws", align_bytes=64)
-
-            def tern(h):
-                cols = slice(2048 * h, 2048 * h + 2048)
-                nc.vector.tensor_scalar(
-                    out=tw[:, cols], in0=mwT[:, cols], scalar1=thr[:, 0:1], scalar2=scl[:, 0:1],
-                    op0=ALU.is_gt, op1=ALU.mult,
-                )
-                nc.vector.tensor_scalar(
-                    out=neg[:], in0=mwT[:, cols], scalar1=nthr[:, 0:1], scalar2=scl[:, 0:1],
-                    op0=ALU.is_lt, op1=ALU.mult,
-                )
+            else:
                 nc.vector.tensor_tensor(
-                    out=tw[:, cols], in0=tw[:, cols], in1=neg[:], op=ALU.subtract
+                    out=ob[:, i, cols], in0=acc[:], in1=bias_sb[:, cols], op=ALU.add
                 )
 
-            def tw_quant(h):
-                nc.vector.quantize_mx(
-                    out=twc[:, 512 * h : 512 * h + 512].bitcast(FP8X4),
-                    scales=tws[:, 512 * h : 512 * h + 512],
-                    in_=tw[:, 2048 * h : 2048 * h + 2048],
-                )
-
-            obs = {}
-            first_of = {}
-            size_of = {}
-            t0 = 0
-            for g in GROUPS:
-                for i in range(g):
-                    first_of[t0 + i] = t0
-                size_of[t0] = g
-                t0 += g
-
-            def unit(t, h):
-                f = first_of[t]
-                if f not in obs:
-                    g = size_of[f]
-                    obs[f] = pools.get(g, outp).tile(
-                        [P, g, N], F32, name="ob%d" % g, tag="ob%d" % g, bufs=OB_BUFS[g]
-                    )
-                ob = obs[f]
-                i = t - f
-                j, tl = divmod(t, TPC)
-                cols = slice(512 * h, 512 * h + 512)
-                acc = accp.tile([P, 512], F32, name="acc", tag="acc")
-                nc.tensor.matmul_mx(
-                    out=acc[:],
-                    lhsT=xc[j][:, P * tl : P * tl + P].bitcast(FP8X4),
-                    lhsT_scale=xs[j][:, P * tl : P * tl + P],
-                    rhs=twc[:, cols].bitcast(FP8X4),
-                    rhs_scale=tws[:, cols],
-                    start=True,
-                    stop=True,
-                )
-                if on_scalar_and_gpsimd(t, h):
-                    nc.scalar.copy(out=ob[:, i, cols], in_=acc[:])
-                    nc.gpsimd.tensor_tensor(
-                        out=ob[:, i, cols], in0=ob[:, i, cols], in1=bias_sb[:, cols], op=ALU.add
-                    )
-                else:
-                    nc.vector.tensor_tensor(
-                        out=ob[:, i, cols], in0=acc[:], in1=bias_sb[:, cols], op=ALU.add
-                    )
-
-            tern(0)
-            x_quant(0, 0, 1)
-            tw_quant(0)
-            x_quant(0, 1, 1)
-            unit(0, 0)
-            bias_s(1)
-            for t in range(1, EARLY):
-                unit(t, 0)
-            for b in (2, 3):
-                x_bank_t(0, b)
-                x_bank_s(0, b)
-            tern(1)
-            tw_quant(1)
-        pools[4] = ctx.enter_context(tc.tile_pool(name="big", bufs=1))
+        tern(0)
+        x_quant(0, 0, 1)
+        tw_quant(0)
+        x_quant(0, 1, 1)
+        unit(0, 0)
+        bias_s(1)
+        for t in range(1, EARLY):
+            unit(t, 0)
+        for b in (2, 3):
+            x_bank_t(0, b)
+            x_bank_s(0, b)
+        tern(1)
+        tw_quant(1)
 
         for t in range(MT):
             if t >= EARLY:

@@ -22,20 +22,21 @@ MT = M // P
 WT = N // P
 XCH = 4
 TPC = MT // XCH
-GROUPS = [1, 1, 1, 1, 2, 2, 2, 2, 4, 4, 4, 4, 2, 1, 1]
-OB_BUFS = {1: 4, 2: 4, 4: 3}
-EARLY = 3
+EARLY = 8
+GROUPS = [1] * (EARLY + 2) + [2] * 10 + [1, 1]
+OB_BUFS = {1: 8, 2: 6}
 
 
 def on_scalar_and_gpsimd(t, h):
-    if t < EARLY:
-        return h == 0
-    return (2 * t + h) % 16 in (1, 4, 7, 10, 13) and t < MT - 2
+    if t < EARLY and h == 0:
+        return t in (1, 3, 7)
+    return (2 * t + h) % 3 == 2 and t < MT - 2
 
 
 def tile_masklockedlinear_t_kernel(tc, x, weight, mask, bias, out):
     nc = tc.nc
     with ExitStack() as ctx:
+        ctx.enter_context(tc.manual_schedule())
         const = ctx.enter_context(tc.tile_pool(name="const", bufs=1))
         outp = ctx.enter_context(tc.tile_pool(name="outp", bufs=1))
         xgp = ctx.enter_context(tc.tile_pool(name="xgp", bufs=2))
@@ -54,8 +55,10 @@ def tile_masklockedlinear_t_kernel(tc, x, weight, mask, bias, out):
         nc.vector.memset(ones_b[:], 1.0)
         ones_f = const.tile([P, P], F32, name="ones_f")
         nc.vector.memset(ones_f[:], 1.0)
-        stats = const.tile([P, 40], F32, name="stats")
-        nc.vector.memset(stats[:], 0.0)
+        stats = const.tile([P, 4], F32, name="stats")
+        stats_s = const.tile([P, 2], F32, name="stats_s")
+        nc.vector.memset(stats_s[:], 0.0)
+        stats_v = const.tile([P, 2], F32, name="stats_v")
 
         w_v = weight.rearrange("(c p a) k -> c p a k", c=4, p=P, a=2)
         m_v = mask.rearrange("(c p a) k -> c p a k", c=4, p=P, a=2)
@@ -73,89 +76,13 @@ def tile_masklockedlinear_t_kernel(tc, x, weight, mask, bias, out):
         x_sb = []
         for j in range(XCH):
             x_c = const.tile([P, TPC * K], BF16, name="x%d" % j)
-            nc.sync.dma_start(
-                out=x_c[:].rearrange("p (t k) -> p t k", t=TPC),
-                in_=x_v[:, TPC * j : TPC * j + TPC, :],
-            )
+            step = TPC // 2 if j == 0 else TPC
+            for i in range(0, TPC, step):
+                nc.sync.dma_start(
+                    out=x_c[:, K * i : K * (i + step)].rearrange("p (t k) -> p t k", t=step),
+                    in_=x_v[:, TPC * j + i : TPC * j + i + step, :],
+                )
             x_sb.append(x_c)
-
-        mwT = const.tile([P, 4 * N], BF16, name="mwT", align_bytes=64)
-        mwT32 = mwT[:].bitcast(F32).rearrange("q (c p a u) -> q c p a u", c=4, p=P, a=2, u=2)
-        junk = const.tile([P, 2, K], BF16, name="junk")
-        gram = tp.tile([P, P], F32, name="gram", tag="tp")
-        tot = tp.tile([P, 2], F32, name="tot", tag="tp")
-
-        def stat_mm(i, first, last):
-            nc.tensor.matmul(
-                tot[:], lhsT=ones_f[:], rhs=stats[:, 8 * i : 8 * i + 2], start=first, stop=last
-            )
-
-        mws, pts = [], {}
-
-        def mw_transposes(c):
-            mw32 = mws[c][:].rearrange("p t k -> p (t k)").bitcast(F32)
-            pt = accp.tile([P, 2, 2, P], F32, name="pt", tag="acc")
-            for a in range(2):
-                for u in range(2):
-                    o = 256 * a + P * u
-                    nc.tensor.transpose(pt[:, a, u, :], mw32[:, o : o + P], ident[:])
-            pts[c] = pt
-
-        def mw_exit(c, engine):
-            src = pts[c][:].rearrange("q a u p -> q p a u")
-            if engine == "v":
-                nc.vector.tensor_copy(out=mwT32[:, c], in_=src)
-            else:
-                nc.scalar.copy(out=mwT32[:, c], in_=src)
-
-        for c in range(4):
-            mw_c = const.tile([P, 2, K], BF16, name="mw%d" % c)
-            mws.append(mw_c)
-            nc.vector.tensor_tensor(out=mw_c[:], in0=w_sb[c][:], in1=m_sb[c][:], op=ALU.mult)
-            nc.scalar.activation(
-                out=junk[:], in_=mw_c[:], func=ACT.Abs, accum_out=stats[:, 8 * c : 8 * c + 1]
-            )
-            for a in range(2):
-                for b in range(4):
-                    blk = mw_c[:, a, P * b : P * b + P]
-                    nc.tensor.matmul(
-                        gram[:],
-                        lhsT=blk,
-                        rhs=blk,
-                        start=(c == 0 and a == 0 and b == 0),
-                        stop=(c == 3 and a == 1 and b == 3),
-                    )
-            if c < 2:
-                mw_transposes(c)
-        for c in range(3):
-            stat_mm(c, c == 0, False)
-        mw_exit(0, "v")
-        diag = const.tile([P, P], F32, name="diag")
-        nc.vector.scalar_tensor_tensor(
-            out=diag[:], in0=gram[:], scalar=float(COUNT), in1=ident[:],
-            op0=ALU.mult, op1=ALU.mult, accum_out=stats[:, 33:34],
-        )
-        mw_exit(1, "v")
-        stat_mm(4, False, False)
-        stat_mm(3, False, True)
-
-        nv = const.tile([P, 1], F32, name="nv")
-        nc.vector.tensor_scalar(
-            out=nv[:], in0=tot[:, 0:1], scalar1=tot[:, 0:1], scalar2=tot[:, 1:2],
-            op0=ALU.mult, op1=ALU.subtract,
-        )
-        nvc = const.tile([P, 1], F32, name="nvc")
-        nc.vector.tensor_scalar_min(out=nvc[:], in0=nv[:], scalar1=0.0)
-        thr = const.tile([P, 1], F32, name="thr")
-        nc.scalar.activation(
-            out=thr[:], in_=nvc[:], func=ACT.Sqrt, scale=-1.0 / (4.0 * COUNT * (COUNT - 1.0))
-        )
-        nthr = const.tile([P, 1], F32, name="nthr")
-        nc.scalar.mul(out=nthr[:], in_=thr[:], mul=-1.0)
-        scl = const.tile([P, 1], F32, name="scl")
-        nc.vector.tensor_scalar(
-            out=scl[:], in0=tot[:, 0:1], scalar1=1.0 / COUNT, scalar2=EPS, op0=ALU.mult, op1=ALU.add
-        )
 
         xg, xc, xs = {}, [], []
         for j in range(XCH):
@@ -195,6 +122,113 @@ def tile_masklockedlinear_t_kernel(tc, x, weight, mask, bias, out):
                 x_bank_t(1 + i // 2, b)
                 x_bank_s(1 + i // 2, b)
 
+        mwT = const.tile([P, 4 * N], BF16, name="mwT", align_bytes=64)
+        mwT32 = mwT[:].bitcast(F32).rearrange("q (c p a u) -> q c p a u", c=4, p=P, a=2, u=2)
+        junk = const.tile([P, 2, K], BF16, name="junk")
+        junk_v = const.tile([P, 2, K], BF16, name="junk_v")
+        gram = tp.tile([P, P], F32, name="gram", tag="tp")
+        tot = tp.tile([P, 2], F32, name="tot", tag="tp")
+
+        def stat_mm(src, first, last):
+            nc.tensor.matmul(tot[:], lhsT=ones_f[:], rhs=src, start=first, stop=last)
+
+        mws, pts = [], {}
+
+        def mw_transposes(c):
+            mw32 = mws[c][:].rearrange("p t k -> p (t k)").bitcast(F32)
+            pt = accp.tile([P, 2, 2, P], F32, name="pt", tag="acc")
+            for a in range(2):
+                for u in range(2):
+                    o = 256 * a + P * u
+                    nc.tensor.transpose(pt[:, a, u, :], mw32[:, o : o + P], ident[:])
+            pts[c] = pt
+
+        def mw_exit(c, engine):
+            src = pts[c][:].rearrange("q a u p -> q p a u")
+            if engine == "v":
+                nc.vector.tensor_copy(out=mwT32[:, c], in_=src)
+            else:
+                nc.scalar.copy(out=mwT32[:, c], in_=src)
+
+        def gram_mm(c, a):
+            for b in range(4):
+                blk = mws[c][:, a, P * b : P * b + P]
+                nc.tensor.matmul(
+                    gram[:],
+                    lhsT=blk,
+                    rhs=blk,
+                    start=(c == 0 and a == 0 and b == 0),
+                    stop=(c == 3 and a == 1 and b == 3),
+                )
+
+        def flat(t, lo, hi):
+            return t[:].rearrange("p t k -> p (t k)")[:, lo:hi]
+
+        def abs_scalar(c, lo, hi):
+            nc.scalar.activation(
+                out=flat(junk, lo, hi), in_=flat(mws[c], lo, hi), func=ACT.Abs,
+                accum_out=stats_s[:, 0:1] if c == 3 else stats[:, c : c + 1],
+            )
+
+        def abs_vector(c, lo, hi):
+            v = flat(mws[c], lo, hi)
+            nc.vector.scalar_tensor_tensor(
+                out=flat(junk_v, lo, hi), in0=v, scalar=-1.0, in1=v, op0=ALU.mult, op1=ALU.max,
+                accum_out=stats[:, c : c + 1],
+            )
+
+        def mult(c, lo, hi):
+            nc.vector.tensor_tensor(
+                out=flat(mws[c], lo, hi), in0=flat(w_sb[c], lo, hi), in1=flat(m_sb[c], lo, hi), op=ALU.mult
+            )
+
+        for c in range(4):
+            mws.append(const.tile([P, 2, K], BF16, name="mw%d" % c))
+        for c in range(3):
+            mult(c, 0, 2 * K)
+            abs_scalar(c, 0, 2 * K)
+            gram_mm(c, 0)
+            gram_mm(c, 1)
+            if c < 2:
+                mw_transposes(c)
+        mult(3, 0, K)
+        mult(3, K, 2 * K)
+        abs_scalar(3, 0, K)
+        abs_vector(3, K, 2 * K)
+        gram_mm(3, 0)
+        gram_mm(3, 1)
+        nc.vector.reduce_sum(out=stats_v[:, 0:1], in_=stats[:], axis=AXIS.X)
+        diag = const.tile([P, P], F32, name="diag")
+        nc.vector.scalar_tensor_tensor(
+            out=diag[:], in0=gram[:], scalar=float(COUNT), in1=ident[:],
+            op0=ALU.mult, op1=ALU.mult, accum_out=stats_v[:, 1:2],
+        )
+        x_bank_t(0, 0)
+        stat_mm(stats_s[:], True, False)
+        stat_mm(stats_v[:], False, True)
+        mw_exit(1, "v")
+        x_bank_s(0, 0)
+        mw_exit(0, "s")
+        x_quant(0, 0, 1)
+
+        nv = const.tile([P, 1], F32, name="nv")
+        nc.vector.tensor_scalar(
+            out=nv[:], in0=tot[:, 0:1], scalar1=tot[:, 0:1], scalar2=tot[:, 1:2],
+            op0=ALU.mult, op1=ALU.subtract,
+        )
+        nvc = const.tile([P, 1], F32, name="nvc")
+        nc.vector.tensor_scalar_min(out=nvc[:], in0=nv[:], scalar1=0.0)
+        thr = const.tile([P, 1], F32, name="thr")
+        nc.scalar.activation(
+            out=thr[:], in_=nvc[:], func=ACT.Sqrt, scale=-1.0 / (4.0 * COUNT * (COUNT - 1.0))
+        )
+        nthr = const.tile([P, 1], F32, name="nthr")
+        nc.scalar.mul(out=nthr[:], in_=thr[:], mul=-1.0)
+        scl = const.tile([P, 1], F32, name="scl")
+        nc.vector.tensor_scalar(
+            out=scl[:], in0=tot[:, 0:1], scalar1=1.0 / COUNT, scalar2=EPS, op0=ALU.mult, op1=ALU.add
+        )
+
         bias_sb = const.tile([P, N], F32, name="bias_sb")
         pbs = {}
 
@@ -208,33 +242,41 @@ def tile_masklockedlinear_t_kernel(tc, x, weight, mask, bias, out):
         def bias_s(h):
             nc.scalar.copy(out=bias_sb[:, 512 * h : 512 * h + 512], in_=pbs[h][:])
 
-        x_bank_t(0, 0)
         x_bank_t(0, 1)
         mw_transposes(2)
         mw_transposes(3)
-        bias_t(0)
-        bias_t(1)
-        x_bank_s(0, 0)
         x_bank_s(0, 1)
         mw_exit(2, "s")
         mw_exit(3, "s")
+        for b in (2, 3):
+            x_bank_t(0, b)
+            x_bank_s(0, b)
+        bias_t(0)
         bias_s(0)
+        bias_t(1)
+        bias_s(1)
 
         tw = const.tile([P, 4 * N], BF16, name="tw", align_bytes=64)
         neg = const.tile([P, 2 * N], BF16, name="neg")
         twc = const.tile([P, N], U32, name="twc", align_bytes=64)
         tws = const.tile([P, N], U8, name="tws", align_bytes=64)
 
-        def tern(h):
+        def tern_pos(h):
             cols = slice(2048 * h, 2048 * h + 2048)
             nc.vector.tensor_scalar(
                 out=tw[:, cols], in0=mwT[:, cols], scalar1=thr[:, 0:1], scalar2=scl[:, 0:1],
                 op0=ALU.is_gt, op1=ALU.mult,
             )
+
+        def tern_neg(h):
+            cols = slice(2048 * h, 2048 * h + 2048)
             nc.vector.tensor_scalar(
                 out=neg[:], in0=mwT[:, cols], scalar1=nthr[:, 0:1], scalar2=scl[:, 0:1],
                 op0=ALU.is_lt, op1=ALU.mult,
             )
+
+        def tern_sub(h):
+            cols = slice(2048 * h, 2048 * h + 2048)
             nc.vector.tensor_tensor(
                 out=tw[:, cols], in0=tw[:, cols], in1=neg[:], op=ALU.subtract
             )
@@ -285,33 +327,55 @@ def tile_masklockedlinear_t_kernel(tc, x, weight, mask, bias, out):
                     out=ob[:, i, cols], in0=acc[:], in1=bias_sb[:, cols], op=ALU.add
                 )
 
-        tern(0)
-        x_quant(0, 0, 1)
+        def store_half(t, h):
+            cols = slice(512 * h, 512 * h + 512)
+            nc.sync.dma_start(out=out_v[:, t, cols], in_=obs[t][:, 0, cols])
+
+        tern_pos(0)
+        tern_neg(0)
+        tern_sub(0)
         tw_quant(0)
         x_quant(0, 1, 1)
+        x_quant(0, 2, 2)
         unit(0, 0)
-        bias_s(1)
-        for t in range(1, EARLY):
-            unit(t, 0)
-        for b in (2, 3):
-            x_bank_t(0, b)
-            x_bank_s(0, b)
-        tern(1)
+        unit(1, 0)
+        unit(2, 0)
+        unit(3, 0)
+        tern_pos(1)
+        unit(4, 0)
+        for t in (0, 2, 4, 1):
+            store_half(t, 0)
+        tern_neg(1)
+        x_bank_t(1, 0)
+        x_bank_s(1, 0)
+        unit(5, 0)
+        tern_sub(1)
+        x_bank_t(1, 1)
+        x_bank_s(1, 1)
+        unit(7, 0)
         tw_quant(1)
+        unit(6, 0)
+        for t in (5, 3, 7, 6):
+            store_half(t, 0)
+        x_quant(1, 0, 2)
+        for t in range(EARLY):
+            unit(t, 1)
+            store_half(t, 1)
+            if t == 1:
+                x_pair(1)
+            if t == 5:
+                x_quant(1, 2, 2)
+                x_pair(2)
 
-        for t in range(MT):
-            if t >= EARLY:
-                unit(t, 0)
+        for t in range(EARLY, MT):
+            unit(t, 0)
             unit(t, 1)
             f = first_of[t]
             if t == f + size_of[f] - 1:
                 g = size_of[f]
                 nc.sync.dma_start(out=out_v[:, f : f + g, :], in_=obs[f][:, 0:g, :])
-            if t == 1:
-                x_quant(0, 2, 2)
-                x_pair(0)
-            if t % 4 == 3 and t // 4 + 1 < 6:
-                x_pair(t // 4 + 1)
-            if t == 3 or (t % 4 == 1 and 1 <= t // 4 < 6):
-                i = t // 4 if t != 3 else 0
+            i = t // 4
+            if t % 4 == 3 and i + 1 < 6:
+                x_pair(i + 1)
+            if t % 4 == 1 and i < 6:
                 x_quant(1 + i // 2, 2 * (i % 2), 2)

@@ -22,15 +22,6 @@ MT = M // P
 WT = N // P
 XCH = 4
 TPC = MT // XCH
-EARLY = 8
-GROUPS = [1] * (EARLY + 2) + [2] * 10 + [1, 1]
-OB_BUFS = {1: 8, 2: 6}
-
-
-def on_scalar_and_gpsimd(t, h):
-    if t < EARLY and h == 0:
-        return t in (1, 3, 7)
-    return (2 * t + h) % 3 == 2 and t < MT - 2
 
 
 def tile_masklockedlinear_t_kernel(tc, x, weight, mask, bias, out):
@@ -207,14 +198,17 @@ def tile_masklockedlinear_t_kernel(tc, x, weight, mask, bias, out):
         stat_mm(stats_s[:], True, False)
         stat_mm(stats_v[:], False, True)
         mw_exit(1, "v")
-        x_bank_s(0, 0)
         mw_exit(0, "s")
-        x_quant(0, 0, 1)
+        x_bank_s(0, 0)
 
         nv = const.tile([P, 1], F32, name="nv")
         nc.vector.tensor_scalar(
             out=nv[:], in0=tot[:, 0:1], scalar1=tot[:, 0:1], scalar2=tot[:, 1:2],
             op0=ALU.mult, op1=ALU.subtract,
+        )
+        scl = const.tile([P, 1], F32, name="scl")
+        nc.vector.tensor_scalar(
+            out=scl[:], in0=tot[:, 0:1], scalar1=1.0 / COUNT, scalar2=EPS, op0=ALU.mult, op1=ALU.add
         )
         nvc = const.tile([P, 1], F32, name="nvc")
         nc.vector.tensor_scalar_min(out=nvc[:], in0=nv[:], scalar1=0.0)
@@ -224,10 +218,6 @@ def tile_masklockedlinear_t_kernel(tc, x, weight, mask, bias, out):
         )
         nthr = const.tile([P, 1], F32, name="nthr")
         nc.scalar.mul(out=nthr[:], in_=thr[:], mul=-1.0)
-        scl = const.tile([P, 1], F32, name="scl")
-        nc.vector.tensor_scalar(
-            out=scl[:], in0=tot[:, 0:1], scalar1=1.0 / COUNT, scalar2=EPS, op0=ALU.mult, op1=ALU.add
-        )
 
         bias_sb = const.tile([P, N], F32, name="bias_sb")
         pbs = {}
@@ -257,7 +247,7 @@ def tile_masklockedlinear_t_kernel(tc, x, weight, mask, bias, out):
         bias_s(1)
 
         tw = const.tile([P, 4 * N], BF16, name="tw", align_bytes=64)
-        neg = const.tile([P, 2 * N], BF16, name="neg")
+        negs = [const.tile([P, 2 * N], BF16, name="neg%d" % h) for h in range(2)]
         twc = const.tile([P, N], U32, name="twc", align_bytes=64)
         tws = const.tile([P, N], U8, name="tws", align_bytes=64)
 
@@ -271,14 +261,14 @@ def tile_masklockedlinear_t_kernel(tc, x, weight, mask, bias, out):
         def tern_neg(h):
             cols = slice(2048 * h, 2048 * h + 2048)
             nc.vector.tensor_scalar(
-                out=neg[:], in0=mwT[:, cols], scalar1=nthr[:, 0:1], scalar2=scl[:, 0:1],
+                out=negs[h][:], in0=mwT[:, cols], scalar1=nthr[:, 0:1], scalar2=scl[:, 0:1],
                 op0=ALU.is_lt, op1=ALU.mult,
             )
 
         def tern_sub(h):
             cols = slice(2048 * h, 2048 * h + 2048)
             nc.vector.tensor_tensor(
-                out=tw[:, cols], in0=tw[:, cols], in1=neg[:], op=ALU.subtract
+                out=tw[:, cols], in0=tw[:, cols], in1=negs[h][:], op=ALU.subtract
             )
 
         def tw_quant(h):
@@ -289,22 +279,18 @@ def tile_masklockedlinear_t_kernel(tc, x, weight, mask, bias, out):
             )
 
         obs = {}
-        first_of = {}
-        size_of = {}
-        t0 = 0
-        for g in GROUPS:
-            for i in range(g):
-                first_of[t0 + i] = t0
-            size_of[t0] = g
-            t0 += g
+        gate = const.tile([P, 1], U32, name="gate")
 
-        def unit(t, h):
-            f = first_of[t]
+        def out_tile(t):
+            g = 1 if t < TPC or t >= MT - 2 else 2
+            f = t - t % g
             if f not in obs:
-                g = size_of[f]
-                obs[f] = outp.tile([P, g, N], F32, name="ob%d" % g, tag="ob%d" % g, bufs=OB_BUFS[g])
-            ob = obs[f]
-            i = t - f
+                obs[f] = outp.tile([P, g, N], F32, name="ob%d" % g, tag="ob%d" % g, bufs=8 if g == 1 else 6)
+            return obs[f], t - f
+
+        accs = {}
+
+        def product(t, h):
             j, tl = divmod(t, TPC)
             cols = slice(512 * h, 512 * h + 512)
             acc = accp.tile([P, 512], F32, name="acc", tag="acc")
@@ -317,65 +303,106 @@ def tile_masklockedlinear_t_kernel(tc, x, weight, mask, bias, out):
                 start=True,
                 stop=True,
             )
-            if on_scalar_and_gpsimd(t, h):
-                nc.scalar.copy(out=ob[:, i, cols], in_=acc[:])
-                nc.gpsimd.tensor_tensor(
-                    out=ob[:, i, cols], in0=ob[:, i, cols], in1=bias_sb[:, cols], op=ALU.add
-                )
-            else:
-                nc.vector.tensor_tensor(
-                    out=ob[:, i, cols], in0=acc[:], in1=bias_sb[:, cols], op=ALU.add
-                )
+            accs[(t, h)] = acc
 
-        def store_half(t, h):
+        def leave_v(t, h):
             cols = slice(512 * h, 512 * h + 512)
-            nc.sync.dma_start(out=out_v[:, t, cols], in_=obs[t][:, 0, cols])
+            ob, i = out_tile(t)
+            nc.vector.tensor_tensor(
+                out=ob[:, i, cols], in0=accs[(t, h)][:], in1=bias_sb[:, cols], op=ALU.add
+            )
 
+        def leave_s(t, h):
+            cols = slice(512 * h, 512 * h + 512)
+            ob, i = out_tile(t)
+            nc.scalar.copy(out=ob[:, i, cols], in_=accs[(t, h)][:])
+
+        def add_g(t, h):
+            cols = slice(512 * h, 512 * h + 512)
+            ob, i = out_tile(t)
+            nc.gpsimd.tensor_tensor(
+                out=ob[:, i, cols], in0=ob[:, i, cols], in1=bias_sb[:, cols], op=ALU.add
+            )
+
+        def store(t, g):
+            ob, i = out_tile(t)
+            nc.sync.dma_start(out=out_v[:, t : t + g, :], in_=ob[:, i : i + g, :])
+
+        x_quant(0, 0, 1)
         tern_pos(0)
         tern_neg(0)
-        tern_sub(0)
-        tw_quant(0)
         x_quant(0, 1, 1)
-        x_quant(0, 2, 2)
-        unit(0, 0)
-        unit(1, 0)
-        unit(2, 0)
-        unit(3, 0)
+        tern_sub(0)
         tern_pos(1)
-        unit(4, 0)
-        for t in (0, 2, 4, 1):
-            store_half(t, 0)
+        tw_quant(0)
+        for t in range(4):
+            product(t, 0)
+            leave_s(t, 0)
         tern_neg(1)
-        x_bank_t(1, 0)
-        x_bank_s(1, 0)
-        unit(5, 0)
+        x_quant(0, 2, 2)
+        product(4, 0)
+        leave_s(4, 0)
         tern_sub(1)
-        x_bank_t(1, 1)
-        x_bank_s(1, 1)
-        unit(7, 0)
+        product(5, 0)
+        product(6, 0)
         tw_quant(1)
-        unit(6, 0)
-        for t in (5, 3, 7, 6):
-            store_half(t, 0)
-        x_quant(1, 0, 2)
-        for t in range(EARLY):
-            unit(t, 1)
-            store_half(t, 1)
-            if t == 1:
-                x_pair(1)
-            if t == 5:
-                x_quant(1, 2, 2)
-                x_pair(2)
+        nc.gpsimd.tensor_copy(out=gate[:], in_=twc[:, N - 1 : N])
+        for t in range(5):
+            add_g(t, 0)
+        leave_v(5, 0)
+        leave_v(6, 0)
+        for t in range(5):
+            product(t, 1)
+            leave_v(t, 1)
+            if t == 3:
+                for b in range(4):
+                    x_bank_t(1, b)
+                    x_bank_s(1, b)
+        store(0, 1)
+        store(1, 1)
+        store(2, 1)
+        for t in (5, 6):
+            product(t, 1)
+            leave_v(t, 1)
+        store(5, 1)
+        store(3, 1)
+        store(6, 1)
+        store(4, 1)
+        product(7, 0)
+        product(7, 1)
+        x_quant(1, 0, 4)
+        leave_v(7, 0)
+        leave_v(7, 1)
+        store(7, 1)
 
-        for t in range(EARLY, MT):
-            unit(t, 0)
-            unit(t, 1)
-            f = first_of[t]
-            if t == f + size_of[f] - 1:
-                g = size_of[f]
-                nc.sync.dma_start(out=out_v[:, f : f + g, :], in_=obs[f][:, 0:g, :])
-            i = t // 4
-            if t % 4 == 3 and i + 1 < 6:
-                x_pair(i + 1)
-            if t % 4 == 1 and i < 6:
-                x_quant(1 + i // 2, 2 * (i % 2), 2)
+        for j in range(1, XCH):
+            c0 = TPC * j
+            last = j == XCH - 1
+            order = [(0, 0), (0, 1), (1, 0), (1, 1), (4, 0), (2, 0), (4, 1), (3, 0),
+                     (2, 1), (5, 0), (5, 1), (3, 1), (6, 0), (6, 1), (7, 0), (7, 1)]
+            for n, (i, h) in enumerate(order):
+                t = c0 + i
+                product(t, h)
+                if i < 4 and h == 0:
+                    leave_s(t, h)
+                    add_g(t, h)
+                else:
+                    if (i, h) == (7, 0) and not last:
+                        x_quant(j + 1, 0, 4)
+                    leave_v(t, h)
+                if n == 8 and not last:
+                    for b in range(4):
+                        x_bank_t(j + 1, b)
+                        x_bank_s(j + 1, b)
+                if (i, h) == (2, 1):
+                    store(c0, 2)
+                if (i, h) == (6, 0):
+                    store(c0 + 4, 2)
+                if (i, h) == (7, 0):
+                    store(c0 + 2, 2)
+                    if last:
+                        store(c0 + 6, 1)
+            if last:
+                store(c0 + 7, 1)
+            else:
+                store(c0 + 6, 2)

@@ -279,7 +279,6 @@ def tile_masklockedlinear_t_kernel(tc, x, weight, mask, bias, out):
             )
 
         obs = {}
-        gate = const.tile([P, 1], U32, name="gate")
 
         def out_tile(t):
             g = 1 if t < TPC or t >= MT - 2 else 2
@@ -312,18 +311,6 @@ def tile_masklockedlinear_t_kernel(tc, x, weight, mask, bias, out):
                 out=ob[:, i, cols], in0=accs[(t, h)][:], in1=bias_sb[:, cols], op=ALU.add
             )
 
-        def leave_s(t, h):
-            cols = slice(512 * h, 512 * h + 512)
-            ob, i = out_tile(t)
-            nc.scalar.copy(out=ob[:, i, cols], in_=accs[(t, h)][:])
-
-        def add_g(t, h):
-            cols = slice(512 * h, 512 * h + 512)
-            ob, i = out_tile(t)
-            nc.gpsimd.tensor_tensor(
-                out=ob[:, i, cols], in0=ob[:, i, cols], in1=bias_sb[:, cols], op=ALU.add
-            )
-
         def store(t, g):
             ob, i = out_tile(t)
             nc.sync.dma_start(out=out_v[:, t : t + g, :], in_=ob[:, i : i + g, :])
@@ -335,74 +322,27 @@ def tile_masklockedlinear_t_kernel(tc, x, weight, mask, bias, out):
         tern_sub(0)
         tern_pos(1)
         tw_quant(0)
-        for t in range(4):
-            product(t, 0)
-            leave_s(t, 0)
+        product(0, 0)
+        product(1, 0)
         tern_neg(1)
         x_quant(0, 2, 2)
-        product(4, 0)
-        leave_s(4, 0)
         tern_sub(1)
-        product(5, 0)
-        product(6, 0)
         tw_quant(1)
-        nc.gpsimd.tensor_copy(out=gate[:], in_=twc[:, N - 1 : N])
-        for t in range(5):
-            add_g(t, 0)
-        leave_v(5, 0)
-        leave_v(6, 0)
-        for t in range(5):
-            product(t, 1)
-            leave_v(t, 1)
-            if t == 3:
-                for b in range(4):
-                    x_bank_t(1, b)
-                    x_bank_s(1, b)
-        store(0, 1)
-        store(1, 1)
-        store(2, 1)
-        for t in (5, 6):
-            product(t, 1)
-            leave_v(t, 1)
-        store(5, 1)
-        store(3, 1)
-        store(6, 1)
-        store(4, 1)
-        product(7, 0)
-        product(7, 1)
-        x_quant(1, 0, 4)
-        leave_v(7, 0)
-        leave_v(7, 1)
-        store(7, 1)
-
-        for j in range(1, XCH):
-            c0 = TPC * j
-            last = j == XCH - 1
-            order = [(0, 0), (0, 1), (1, 0), (1, 1), (4, 0), (2, 0), (4, 1), (3, 0),
-                     (2, 1), (5, 0), (5, 1), (3, 1), (6, 0), (6, 1), (7, 0), (7, 1)]
-            for n, (i, h) in enumerate(order):
-                t = c0 + i
-                product(t, h)
-                if i < 4 and h == 0:
-                    leave_s(t, h)
-                    add_g(t, h)
-                else:
-                    if (i, h) == (7, 0) and not last:
-                        x_quant(j + 1, 0, 4)
-                    leave_v(t, h)
-                if n == 8 and not last:
-                    for b in range(4):
-                        x_bank_t(j + 1, b)
-                        x_bank_s(j + 1, b)
-                if (i, h) == (2, 1):
-                    store(c0, 2)
-                if (i, h) == (6, 0):
-                    store(c0 + 4, 2)
-                if (i, h) == (7, 0):
-                    store(c0 + 2, 2)
-                    if last:
-                        store(c0 + 6, 1)
-            if last:
-                store(c0 + 7, 1)
-            else:
-                store(c0 + 6, 2)
+        units = [(0, 0), (1, 0), (0, 1), (1, 1)] + [(t, h) for t in range(2, MT) for h in range(2)]
+        for n, (t, h) in enumerate(units):
+            if n + 2 < len(units):
+                if n + 2 >= 2:
+                    product(*units[n + 2])
+            leave_v(t, h)
+            if h == 1:
+                if t % 2 == 0 and t < MT - TPC:
+                    x_bank_t(1 + t // TPC, t % TPC // 2)
+                    x_bank_s(1 + t // TPC, t % TPC // 2)
+                if t % 8 == 5 and t < MT - TPC:
+                    x_quant(1 + t // TPC, 0, 2)
+                if t % 8 == 1 and t >= TPC:
+                    x_quant(t // TPC, 2, 2)
+                if t < TPC or t >= MT - 2:
+                    store(t, 1)
+                elif t % 2 == 1:
+                    store(t - 1, 2)

@@ -46,15 +46,13 @@ def tile_masklockedlinear_t_kernel(tc, x, weight, mask, bias, out):
         nc.vector.memset(ones_b[:], 1.0)
         ones_f = const.tile([P, P], F32, name="ones_f")
         nc.vector.memset(ones_f[:], 1.0)
-        stats = const.tile([P, 4], F32, name="stats")
-        stats_s = const.tile([P, 2], F32, name="stats_s")
-        nc.vector.memset(stats_s[:], 0.0)
-        stats_v = const.tile([P, 2], F32, name="stats_v")
+        stats = const.tile([P, 6], F32, name="stats")
 
         w_v = weight.rearrange("(c p a) k -> c p a k", c=4, p=P, a=2)
         m_v = mask.rearrange("(c p a) k -> c p a k", c=4, p=P, a=2)
         x_v = x.rearrange("(p t) k -> p t k", t=MT)
         out_v = out.rearrange("(p t) n -> p t n", t=MT)
+        nc.scalar.dma_start(out=bias_row[0:1, :], in_=bias.rearrange("(o n) -> o n", o=1))
         w_sb, m_sb = [], []
         for c in range(4):
             w_c = const.tile([P, 2, K], BF16, name="w%d" % c)
@@ -63,7 +61,6 @@ def tile_masklockedlinear_t_kernel(tc, x, weight, mask, bias, out):
             nc.sync.dma_start(out=m_c[:], in_=m_v[c])
             w_sb.append(w_c)
             m_sb.append(m_c)
-        nc.sync.dma_start(out=bias_row[0:1, :], in_=bias.rearrange("(o n) -> o n", o=1))
         x_sb = []
         for j in range(XCH):
             x_c = const.tile([P, TPC * K], BF16, name="x%d" % j)
@@ -115,14 +112,30 @@ def tile_masklockedlinear_t_kernel(tc, x, weight, mask, bias, out):
 
         mwT = const.tile([P, 4 * N], BF16, name="mwT", align_bytes=64)
         mwT32 = mwT[:].bitcast(F32).rearrange("q (c p a u) -> q c p a u", c=4, p=P, a=2, u=2)
-        junk = const.tile([P, 2, K], BF16, name="junk")
-        junk_v = const.tile([P, 2, K], BF16, name="junk_v")
+        junk = [const.tile([P, 2, K], BF16, name="junk%d" % c) for c in range(5)]
         gram = tp.tile([P, P], F32, name="gram", tag="tp")
-        tot = tp.tile([P, 2], F32, name="tot", tag="tp")
+        tot1 = accp.tile([P, 1], F32, name="tot1", tag="acc")
+        tot2 = accp.tile([P, 1], F32, name="tot2", tag="acc")
 
-        def stat_mm(src, first, last):
+        def sum_mm(tot, src, first, last):
             nc.tensor.matmul(tot[:], lhsT=ones_f[:], rhs=src, start=first, stop=last)
 
+        bias_sb = const.tile([P, N], F32, name="bias_sb")
+        pbs = {}
+
+        def bias_t(h):
+            pb = accp.tile([P, 512], F32, name="pb", tag="acc")
+            nc.tensor.matmul(
+                pb[:], lhsT=ones_b[:], rhs=bias_row[:, 512 * h : 512 * h + 512], start=True, stop=True
+            )
+            pbs[h] = pb
+
+        def bias_s(h):
+            nc.scalar.copy(out=bias_sb[:, 512 * h : 512 * h + 512], in_=pbs[h][:])
+
+        for h in range(2):
+            bias_t(h)
+            bias_s(h)
         mws, pts = [], {}
 
         def mw_transposes(c):
@@ -157,15 +170,15 @@ def tile_masklockedlinear_t_kernel(tc, x, weight, mask, bias, out):
 
         def abs_scalar(c, lo, hi):
             nc.scalar.activation(
-                out=flat(junk, lo, hi), in_=flat(mws[c], lo, hi), func=ACT.Abs,
-                accum_out=stats_s[:, 0:1] if c == 3 else stats[:, c : c + 1],
+                out=flat(junk[c], lo, hi), in_=flat(mws[c], lo, hi), func=ACT.Abs,
+                accum_out=stats[:, c : c + 1],
             )
 
         def abs_vector(c, lo, hi):
             v = flat(mws[c], lo, hi)
             nc.vector.scalar_tensor_tensor(
-                out=flat(junk_v, lo, hi), in0=v, scalar=-1.0, in1=v, op0=ALU.mult, op1=ALU.max,
-                accum_out=stats[:, c : c + 1],
+                out=flat(junk[4], lo, hi), in0=v, scalar=-1.0, in1=v, op0=ALU.mult, op1=ALU.max,
+                accum_out=stats[:, 4:5],
             )
 
         def mult(c, lo, hi):
@@ -182,69 +195,56 @@ def tile_masklockedlinear_t_kernel(tc, x, weight, mask, bias, out):
             gram_mm(c, 1)
             if c < 2:
                 mw_transposes(c)
+                sum_mm(tot1, stats[:, c : c + 1], c == 0, False)
         mult(3, 0, K)
         mult(3, K, 2 * K)
-        abs_scalar(3, 0, K)
-        abs_vector(3, K, 2 * K)
+        abs_vector(3, 0, K)
+        abs_scalar(3, K, 2 * K)
         gram_mm(3, 0)
         gram_mm(3, 1)
-        nc.vector.reduce_sum(out=stats_v[:, 0:1], in_=stats[:], axis=AXIS.X)
+        sum_mm(tot1, stats[:, 2:3], False, False)
+        sum_mm(tot1, stats[:, 4:5], False, False)
+        sum_mm(tot1, stats[:, 3:4], False, True)
         diag = const.tile([P, P], F32, name="diag")
         nc.vector.scalar_tensor_tensor(
             out=diag[:], in0=gram[:], scalar=float(COUNT), in1=ident[:],
-            op0=ALU.mult, op1=ALU.mult, accum_out=stats_v[:, 1:2],
+            op0=ALU.mult, op1=ALU.mult, accum_out=stats[:, 5:6],
         )
+        sum_mm(tot2, stats[:, 5:6], True, True)
         x_bank_t(0, 0)
-        stat_mm(stats_s[:], True, False)
-        stat_mm(stats_v[:], False, True)
-        mw_exit(1, "v")
         mw_exit(0, "s")
-        x_bank_s(0, 0)
+        mw_exit(1, "v")
 
-        nv = const.tile([P, 1], F32, name="nv")
+        sq1 = const.tile([P, 1], F32, name="sq1")
         nc.vector.tensor_scalar(
-            out=nv[:], in0=tot[:, 0:1], scalar1=tot[:, 0:1], scalar2=tot[:, 1:2],
-            op0=ALU.mult, op1=ALU.subtract,
+            out=sq1[:], in0=tot1[:], scalar1=tot1[:, 0:1], scalar2=None, op0=ALU.mult
         )
         scl = const.tile([P, 1], F32, name="scl")
         nc.vector.tensor_scalar(
-            out=scl[:], in0=tot[:, 0:1], scalar1=1.0 / COUNT, scalar2=EPS, op0=ALU.mult, op1=ALU.add
+            out=scl[:], in0=tot1[:], scalar1=1.0 / COUNT, scalar2=EPS, op0=ALU.mult, op1=ALU.add
         )
         nvc = const.tile([P, 1], F32, name="nvc")
-        nc.vector.tensor_scalar_min(out=nvc[:], in0=nv[:], scalar1=0.0)
+        nc.vector.tensor_scalar(
+            out=nvc[:], in0=tot2[:], scalar1=sq1[:, 0:1], scalar2=sq1[:, 0:1],
+            op0=ALU.max, op1=ALU.subtract,
+        )
         thr = const.tile([P, 1], F32, name="thr")
         nc.scalar.activation(
-            out=thr[:], in_=nvc[:], func=ACT.Sqrt, scale=-1.0 / (4.0 * COUNT * (COUNT - 1.0))
+            out=thr[:], in_=nvc[:], func=ACT.Sqrt, scale=1.0 / (4.0 * COUNT * (COUNT - 1.0))
         )
         nthr = const.tile([P, 1], F32, name="nthr")
         nc.scalar.mul(out=nthr[:], in_=thr[:], mul=-1.0)
 
-        bias_sb = const.tile([P, N], F32, name="bias_sb")
-        pbs = {}
-
-        def bias_t(h):
-            pb = accp.tile([P, 512], F32, name="pb", tag="acc")
-            nc.tensor.matmul(
-                pb[:], lhsT=ones_b[:], rhs=bias_row[:, 512 * h : 512 * h + 512], start=True, stop=True
-            )
-            pbs[h] = pb
-
-        def bias_s(h):
-            nc.scalar.copy(out=bias_sb[:, 512 * h : 512 * h + 512], in_=pbs[h][:])
-
         x_bank_t(0, 1)
         mw_transposes(2)
         mw_transposes(3)
+        x_bank_s(0, 0)
         x_bank_s(0, 1)
         mw_exit(2, "s")
         mw_exit(3, "s")
         for b in (2, 3):
             x_bank_t(0, b)
             x_bank_s(0, b)
-        bias_t(0)
-        bias_s(0)
-        bias_t(1)
-        bias_s(1)
 
         tw = const.tile([P, 4 * N], BF16, name="tw", align_bytes=64)
         negs = [const.tile([P, 2 * N], BF16, name="neg%d" % h) for h in range(2)]
@@ -308,32 +308,48 @@ def tile_masklockedlinear_t_kernel(tc, x, weight, mask, bias, out):
             cols = slice(512 * h, 512 * h + 512)
             ob, i = out_tile(t)
             nc.vector.tensor_tensor(
-                out=ob[:, i, cols], in0=accs[(t, h)][:], in1=bias_sb[:, cols], op=ALU.add
+                out=ob[:, i, cols], in0=bias_sb[:, cols], in1=accs[(t, h)][:], op=ALU.add
+            )
+
+        def leave_sg(t, h):
+            cols = slice(512 * h, 512 * h + 512)
+            ob, i = out_tile(t)
+            nc.scalar.copy(out=ob[:, i, cols], in_=accs[(t, h)][:])
+            nc.gpsimd.tensor_tensor(
+                out=ob[:, i, cols], in0=ob[:, i, cols], in1=bias_sb[:, cols], op=ALU.add
             )
 
         def store(t, g):
             ob, i = out_tile(t)
             nc.sync.dma_start(out=out_v[:, t : t + g, :], in_=ob[:, i : i + g, :])
 
-        x_quant(0, 0, 1)
         tern_pos(0)
         tern_neg(0)
-        x_quant(0, 1, 1)
+        x_quant(0, 0, 1)
         tern_sub(0)
         tern_pos(1)
         tw_quant(0)
         product(0, 0)
         product(1, 0)
         tern_neg(1)
-        x_quant(0, 2, 2)
+        x_quant(0, 1, 1)
         tern_sub(1)
+        product(2, 0)
+        leave_v(0, 0)
         tw_quant(1)
-        units = [(0, 0), (1, 0), (0, 1), (1, 1)] + [(t, h) for t in range(2, MT) for h in range(2)]
+        product(3, 0)
+        leave_v(1, 0)
+        product(0, 1)
+        product(1, 1)
+        units = [(0, 1), (1, 1), (2, 0), (3, 0), (2, 1), (3, 1)] + [(t, h) for t in range(4, MT) for h in range(2)]
+        x_quant(0, 2, 2)
         for n, (t, h) in enumerate(units):
-            if n + 2 < len(units):
-                if n + 2 >= 2:
-                    product(*units[n + 2])
-            leave_v(t, h)
+            if n + 2 < len(units) and units[n + 2] not in ((2, 0), (3, 0)):
+                product(*units[n + 2])
+            if h == 0 and t % 2 == 0 and 2 <= t < 28:
+                leave_sg(t, h)
+            else:
+                leave_v(t, h)
             if h == 1:
                 if t % 2 == 0 and t < MT - TPC:
                     x_bank_t(1 + t // TPC, t % TPC // 2)

@@ -52,7 +52,6 @@ def tile_masklockedlinear_t_kernel(tc, x, weight, mask, bias, out):
         m_v = mask.rearrange("(c p a) k -> c p a k", c=4, p=P, a=2)
         x_v = x.rearrange("(p t) k -> p t k", t=MT)
         out_v = out.rearrange("(p t) n -> p t n", t=MT)
-        nc.scalar.dma_start(out=bias_row[0:1, :], in_=bias.rearrange("(o n) -> o n", o=1))
         w_sb, m_sb = [], []
         for c in range(4):
             w_c = const.tile([P, 2, K], BF16, name="w%d" % c)
@@ -61,6 +60,7 @@ def tile_masklockedlinear_t_kernel(tc, x, weight, mask, bias, out):
             nc.sync.dma_start(out=m_c[:], in_=m_v[c])
             w_sb.append(w_c)
             m_sb.append(m_c)
+        nc.sync.dma_start(out=bias_row[0:1, :], in_=bias.rearrange("(o n) -> o n", o=1))
         x_sb = []
         for j in range(XCH):
             x_c = const.tile([P, TPC * K], BF16, name="x%d" % j)
@@ -133,9 +133,6 @@ def tile_masklockedlinear_t_kernel(tc, x, weight, mask, bias, out):
         def bias_s(h):
             nc.scalar.copy(out=bias_sb[:, 512 * h : 512 * h + 512], in_=pbs[h][:])
 
-        for h in range(2):
-            bias_t(h)
-            bias_s(h)
         mws, pts = [], {}
 
         def mw_transposes(c):
@@ -242,6 +239,9 @@ def tile_masklockedlinear_t_kernel(tc, x, weight, mask, bias, out):
         x_bank_s(0, 1)
         mw_exit(2, "s")
         mw_exit(3, "s")
+        for h in range(2):
+            bias_t(h)
+            bias_s(h)
         for b in (2, 3):
             x_bank_t(0, b)
             x_bank_s(0, b)

@@ -281,7 +281,7 @@ def tile_masklockedlinear_t_kernel(tc, x, weight, mask, bias, out):
         obs = {}
 
         def out_tile(t):
-            g = 1 if t < TPC or t >= MT - 2 else 2
+            g = 1 if t < 6 or t >= MT - 2 else 2
             f = t - t % g
             if f not in obs:
                 obs[f] = outp.tile([P, g, N], F32, name="ob%d" % g, tag="ob%d" % g, bufs=8 if g == 1 else 6)
@@ -323,6 +323,12 @@ def tile_masklockedlinear_t_kernel(tc, x, weight, mask, bias, out):
             ob, i = out_tile(t)
             nc.sync.dma_start(out=out_v[:, t : t + g, :], in_=ob[:, i : i + g, :])
 
+        def store_half(t, h):
+            ob, i = out_tile(t)
+            cols = slice(512 * h, 512 * h + 512)
+            nc.sync.dma_start(out=out_v[:, t, cols], in_=ob[:, i, cols])
+
+        gate = const.tile([P, 1], U32, name="gate")
         tern_pos(0)
         tern_neg(0)
         x_quant(0, 0, 1)
@@ -333,32 +339,56 @@ def tile_masklockedlinear_t_kernel(tc, x, weight, mask, bias, out):
         product(1, 0)
         tern_neg(1)
         x_quant(0, 1, 1)
-        tern_sub(1)
         product(2, 0)
-        leave_v(0, 0)
-        tw_quant(1)
-        product(3, 0)
-        leave_v(1, 0)
-        product(0, 1)
-        product(1, 1)
-        units = [(0, 1), (1, 1), (2, 0), (3, 0), (2, 1), (3, 1)] + [(t, h) for t in range(4, MT) for h in range(2)]
+        tern_sub(1)
         x_quant(0, 2, 2)
+        tw_quant(1)
+        nc.gpsimd.tensor_copy(out=gate[:], in_=twc[:, N - 1 : N])
+        leave_sg(2, 0)
+        product(3, 0)
+        leave_sg(3, 0)
+        for b in range(3):
+            x_bank_t(1, b)
+            x_bank_s(1, b)
+        leave_v(0, 0)
+        store_half(0, 0)
+        leave_v(1, 0)
+        store_half(1, 0)
+        for t in range(3):
+            product(t, 1)
+        for t in range(2):
+            leave_v(t, 1)
+            store_half(t, 1)
+        product(3, 1)
+        product(4, 0)
+        leave_v(2, 1)
+        store(2, 1)
+        product(4, 1)
+        product(5, 0)
+        leave_v(3, 1)
+        store(3, 1)
+        units = [(t, h) for t in range(4, MT) for h in range(2)]
         for n, (t, h) in enumerate(units):
-            if n + 2 < len(units) and units[n + 2] not in ((2, 0), (3, 0)):
+            if 3 <= n + 2 < len(units):
                 product(*units[n + 2])
-            if h == 0 and t % 2 == 0 and 2 <= t < 28:
+            elif n + 2 == 2:
+                pass
+            if h == 0 and t % 2 == 0 and 4 <= t < 28:
                 leave_sg(t, h)
             else:
                 leave_v(t, h)
             if h == 1:
-                if t % 2 == 0 and t < MT - TPC:
+                if 4 <= t < 8-3:
+                    x_bank_t(1, t - 4+3)
+                    x_bank_s(1, t - 4+3)
+                if t % 2 == 0 and TPC <= t < MT - TPC:
                     x_bank_t(1 + t // TPC, t % TPC // 2)
                     x_bank_s(1 + t // TPC, t % TPC // 2)
                 if t % 8 == 5 and t < MT - TPC:
                     x_quant(1 + t // TPC, 0, 2)
                 if t % 8 == 1 and t >= TPC:
                     x_quant(t // TPC, 2, 2)
-                if t < TPC or t >= MT - 2:
+                if t < 6 or t >= MT - 2:
                     store(t, 1)
                 elif t % 2 == 1:
                     store(t - 1, 2)

from contextlib import ExitStack

import concourse.mybir as mybir
from concourse.masks import make_identity

FP8X4 = mybir.dt.float8_e4m3fn_x4
BF16 = mybir.dt.bfloat16
F32 = mybir.dt.float32
U32 = mybir.dt.uint32
U8 = mybir.dt.uint8
ALU = mybir.AluOpType
ACT = mybir.ActivationFunctionType
AXIS = mybir.AxisListType

P = 128
M, K, N = 4096, 512, 1024
EPS = 1e-08
COUNT = N * K
FLOPS = 2 * M * K * N

MT = M // P
WT = N // P
XCH = 4
TPC = MT // XCH


def tile_masklockedlinear_t_kernel(tc, x, weight, mask, bias, out):
    nc = tc.nc
    with ExitStack() as ctx:
        ctx.enter_context(tc.manual_schedule())
        const = ctx.enter_context(tc.tile_pool(name="const", bufs=1))
        outp = ctx.enter_context(tc.tile_pool(name="outp", bufs=1))
        xgp = ctx.enter_context(tc.tile_pool(name="xgp", bufs=2))
        tp = ctx.enter_context(tc.psum_pool(name="tp", bufs=3))
        accp = ctx.enter_context(tc.psum_pool(name="accp", bufs=5))

        bias_row = const.tile([P, N], BF16, name="bias_row")
        nc.vector.memset(bias_row[:], 0.0)
        one_col = const.tile([P, 1], F32, name="one_col")
        nc.vector.memset(one_col[:], 1.0)
        warm = const.tile([P, 1], F32, name="warm")
        nc.scalar.activation(out=warm[:], in_=one_col[:], func=ACT.Sqrt)
        ident = const.tile([P, P], F32, name="ident")
        make_identity(nc, ident[:])
        ones_b = const.tile([P, P], BF16, name="ones_b")
        nc.vector.memset(ones_b[:], 1.0)
        ones_f = const.tile([P, P], F32, name="ones_f")
        nc.vector.memset(ones_f[:], 1.0)
        stats = const.tile([P, 6], F32, name="stats")

        w_v = weight.rearrange("(c p a) k -> c p a k", c=4, p=P, a=2)
        m_v = mask.rearrange("(c p a) k -> c p a k", c=4, p=P, a=2)
        x_v = x.rearrange("(p t) k -> p t k", t=MT)
        out_v = out.rearrange("(p t) n -> p t n", t=MT)
        w_sb, m_sb = [], []
        for c in range(4):
            w_c = const.tile([P, 2, K], BF16, name="w%d" % c)
            nc.sync.dma_start(out=w_c[:], in_=w_v[c])
            m_c = const.tile([P, 2, K], BF16, name="m%d" % c)
            nc.sync.dma_start(out=m_c[:], in_=m_v[c])
            w_sb.append(w_c)
            m_sb.append(m_c)
        nc.sync.dma_start(out=bias_row[0:1, :], in_=bias.rearrange("(o n) -> o n", o=1))
        x_sb = []
        for j in range(XCH):
            x_c = const.tile([P, TPC * K], BF16, name="x%d" % j)
            step = TPC // 2 if j == 0 else TPC
            for i in range(0, TPC, step):
                nc.sync.dma_start(
                    out=x_c[:, K * i : K * (i + step)].rearrange("p (t k) -> p t k", t=step),
                    in_=x_v[:, TPC * j + i : TPC * j + i + step, :],
                )
            x_sb.append(x_c)

        xg, xc, xs = {}, [], []
        for j in range(XCH):
            xc.append(const.tile([P, TPC * P], U32, name="xc%d" % j, align_bytes=64))
            xs.append(const.tile([P, TPC * P], U8, name="xs%d" % j, align_bytes=64))

        xts = {}

        def x_bank_t(j, b):
            x32 = x_sb[j][:].bitcast(F32)
            xt = tp.tile([P, 2, 2, P], F32, name="xt", tag="tp")
            for a in range(2):
                for u in range(2):
                    o = 256 * (2 * b + a) + P * u
                    nc.tensor.transpose(xt[:, a, u, :], x32[:, o : o + P], ident[:])
            xts[(j, b)] = xt

        def x_bank_s(j, b):
            xt = xts[(j, b)]
            if j not in xg:
                xg[j] = xgp.tile([P, TPC * K], BF16, name="xg", tag="xg", align_bytes=64)
            dst = xg[j][:].bitcast(F32)[:, 512 * b : 512 * b + 512]
            nc.scalar.copy(
                out=dst.rearrange("q (a p u) -> q a p u", a=2, p=P, u=2),
                in_=xt[:].rearrange("q a u p -> q a p u"),
            )

        def x_quant(j, b0, nb):
            nc.vector.quantize_mx(
                out=xc[j][:, 256 * b0 : 256 * (b0 + nb)].bitcast(FP8X4),
                scales=xs[j][:, 256 * b0 : 256 * (b0 + nb)],
                in_=xg[j][:, 1024 * b0 : 1024 * (b0 + nb)],
            )

        def x_pair(i):
            for b in (2 * (i % 2), 2 * (i % 2) + 1):
                x_bank_t(1 + i // 2, b)
                x_bank_s(1 + i // 2, b)

        mwT = const.tile([P, 4 * N], BF16, name="mwT", align_bytes=64)
        mwT32 = mwT[:].bitcast(F32).rearrange("q (c p a u) -> q c p a u", c=4, p=P, a=2, u=2)
        junk = [const.tile([P, 2, K], BF16, name="junk%d" % c) for c in range(5)]
        gram = tp.tile([P, P], F32, name="gram", tag="tp")
        tot1 = accp.tile([P, 1], F32, name="tot1", tag="acc")
        tot2 = accp.tile([P, 1], F32, name="tot2", tag="acc")

        def sum_mm(tot, src, first, last):
            nc.tensor.matmul(tot[:], lhsT=ones_f[:], rhs=src, start=first, stop=last)

        bias_sb = const.tile([P, N], F32, name="bias_sb")
        pbs = {}

        def bias_t(h):
            pb = accp.tile([P, 512], F32, name="pb", tag="acc")
            nc.tensor.matmul(
                pb[:], lhsT=ones_b[:], rhs=bias_row[:, 512 * h : 512 * h + 512], start=True, stop=True
            )
            pbs[h] = pb

        def bias_s(h):
            nc.scalar.copy(out=bias_sb[:, 512 * h : 512 * h + 512], in_=pbs[h][:])

        mws, pts = [], {}

        def mw_transposes(c):
            mw32 = mws[c][:].rearrange("p t k -> p (t k)").bitcast(F32)
            pt = accp.tile([P, 2, 2, P], F32, name="pt", tag="acc")
            for a in range(2):
                for u in range(2):
                    o = 256 * a + P * u
                    nc.tensor.transpose(pt[:, a, u, :], mw32[:, o : o + P], ident[:])
            pts[c] = pt

        def mw_exit(c, engine):
            src = pts[c][:].rearrange("q a u p -> q p a u")
            if engine == "v":
                nc.vector.tensor_copy(out=mwT32[:, c], in_=src)
            else:
                nc.scalar.copy(out=mwT32[:, c], in_=src)

        def gram_mm(c, a):
            for b in range(4):
                blk = mws[c][:, a, P * b : P * b + P]
                nc.tensor.matmul(
                    gram[:],
                    lhsT=blk,
                    rhs=blk,
                    start=(c == 0 and a == 0 and b == 0),
                    stop=(c == 3 and a == 1 and b == 3),
                )

        def flat(t, lo, hi):
            return t[:].rearrange("p t k -> p (t k)")[:, lo:hi]

        def abs_scalar(c, lo, hi):
            nc.scalar.activation(
                out=flat(junk[c], lo, hi), in_=flat(mws[c], lo, hi), func=ACT.Abs,
                accum_out=stats[:, c : c + 1],
            )

        def abs_vector(c, lo, hi):
            v = flat(mws[c], lo, hi)
            nc.vector.scalar_tensor_tensor(
                out=flat(junk[4], lo, hi), in0=v, scalar=-1.0, in1=v, op0=ALU.mult, op1=ALU.max,
                accum_out=stats[:, 4:5],
            )

        def mult(c, lo, hi):
            nc.vector.tensor_tensor(
                out=flat(mws[c], lo, hi), in0=flat(w_sb[c], lo, hi), in1=flat(m_sb[c], lo, hi), op=ALU.mult
            )

        for c in range(4):
            mws.append(const.tile([P, 2, K], BF16, name="mw%d" % c))
        for c in range(3):
            mult(c, 0, 2 * K)
            abs_scalar(c, 0, 2 * K)
            gram_mm(c, 0)
            gram_mm(c, 1)
            if c < 2:
                mw_transposes(c)
                sum_mm(tot1, stats[:, c : c + 1], c == 0, False)
        mult(3, 0, K)
        mult(3, K, 2 * K)
        abs_vector(3, 0, K)
        abs_scalar(3, K, 2 * K)
        gram_mm(3, 0)
        gram_mm(3, 1)
        sum_mm(tot1, stats[:, 2:3], False, False)
        sum_mm(tot1, stats[:, 4:5], False, False)
        sum_mm(tot1, stats[:, 3:4], False, True)
        diag = const.tile([P, P], F32, name="diag")
        nc.vector.scalar_tensor_tensor(
            out=diag[:], in0=gram[:], scalar=float(COUNT), in1=ident[:],
            op0=ALU.mult, op1=ALU.mult, accum_out=stats[:, 5:6],
        )
        sum_mm(tot2, stats[:, 5:6], True, True)
        x_bank_t(0, 0)
        mw_exit(0, "s")
        mw_exit(1, "v")

        sq1 = const.tile([P, 1], F32, name="sq1")
        nc.vector.tensor_scalar(
            out=sq1[:], in0=tot1[:], scalar1=tot1[:, 0:1], scalar2=None, op0=ALU.mult
        )
        scl = const.tile([P, 1], F32, name="scl")
        nc.vector.tensor_scalar(
            out=scl[:], in0=tot1[:], scalar1=1.0 / COUNT, scalar2=EPS, op0=ALU.mult, op1=ALU.add
        )
        nvc = const.tile([P, 1], F32, name="nvc")
        nc.vector.tensor_scalar(
            out=nvc[:], in0=tot2[:], scalar1=sq1[:, 0:1], scalar2=sq1[:, 0:1],
            op0=ALU.max, op1=ALU.subtract,
        )
        thr = const.tile([P, 1], F32, name="thr")
        nc.scalar.activation(
            out=thr[:], in_=nvc[:], func=ACT.Sqrt, scale=1.0 / (4.0 * COUNT * (COUNT - 1.0))
        )
        nthr = const.tile([P, 1], F32, name="nthr")
        nc.scalar.mul(out=nthr[:], in_=thr[:], mul=-1.0)

        x_bank_t(0, 1)
        mw_transposes(2)
        mw_transposes(3)
        x_bank_s(0, 0)
        x_bank_s(0, 1)
        mw_exit(2, "s")
        mw_exit(3, "s")
        for h in range(2):
            bias_t(h)
            bias_s(h)
        for b in (2, 3):
            x_bank_t(0, b)
            x_bank_s(0, b)

        tw = const.tile([P, 4 * N], BF16, name="tw", align_bytes=64)
        negs = [const.tile([P, 2 * N], BF16, name="neg%d" % h) for h in range(2)]
        twc = const.tile([P, N], U32, name="twc", align_bytes=64)
        tws = const.tile([P, N], U8, name="tws", align_bytes=64)

        def tern_pos(h):
            cols = slice(2048 * h, 2048 * h + 2048)
            nc.vector.tensor_scalar(
                out=tw[:, cols], in0=mwT[:, cols], scalar1=thr[:, 0:1], scalar2=scl[:, 0:1],
                op0=ALU.is_gt, op1=ALU.mult,
            )

        def tern_neg(h):
            cols = slice(2048 * h, 2048 * h + 2048)
            nc.vector.tensor_scalar(
                out=negs[h][:], in0=mwT[:, cols], scalar1=nthr[:, 0:1], scalar2=scl[:, 0:1],
                op0=ALU.is_lt, op1=ALU.mult,
            )

        def tern_sub(h):
            cols = slice(2048 * h, 2048 * h + 2048)
            nc.vector.tensor_tensor(
                out=tw[:, cols], in0=tw[:, cols], in1=negs[h][:], op=ALU.subtract
            )

        def tw_quant(h):
            nc.vector.quantize_mx(
                out=twc[:, 512 * h : 512 * h + 512].bitcast(FP8X4),
                scales=tws[:, 512 * h : 512 * h + 512],
                in_=tw[:, 2048 * h : 2048 * h + 2048],
            )

        obs = {}

        def out_tile(t):
            g = 1 if t < 6 or t >= MT - 2 else 2
            f = t - t % g
            if f not in obs:
                obs[f] = outp.tile([P, g, N], F32, name="ob%d" % g, tag="ob%d" % g, bufs=8 if g == 1 else 6)
            return obs[f], t - f

        accs = {}

        def product(t, h):
            j, tl = divmod(t, TPC)
            cols = slice(512 * h, 512 * h + 512)
            acc = accp.tile([P, 512], F32, name="acc", tag="acc")
            nc.tensor.matmul_mx(
                out=acc[:],
                lhsT=xc[j][:, P * tl : P * tl + P].bitcast(FP8X4),
                lhsT_scale=xs[j][:, P * tl : P * tl + P],
                rhs=twc[:, cols].bitcast(FP8X4),
                rhs_scale=tws[:, cols],
                start=True,
                stop=True,
            )
            accs[(t, h)] = acc

        def leave_v(t, h):
            cols = slice(512 * h, 512 * h + 512)
            ob, i = out_tile(t)
            nc.vector.tensor_tensor(
                out=ob[:, i, cols], in0=bias_sb[:, cols], in1=accs[(t, h)][:], op=ALU.add
            )

        def leave_sg(t, h):
            cols = slice(512 * h, 512 * h + 512)
            ob, i = out_tile(t)
            nc.scalar.copy(out=ob[:, i, cols], in_=accs[(t, h)][:])
            nc.gpsimd.tensor_tensor(
                out=ob[:, i, cols], in0=ob[:, i, cols], in1=bias_sb[:, cols], op=ALU.add
            )

        def store(t, g):
            ob, i = out_tile(t)
            nc.sync.dma_start(out=out_v[:, t : t + g, :], in_=ob[:, i : i + g, :])

        def store_half(t, h):
            ob, i = out_tile(t)
            cols = slice(512 * h, 512 * h + 512)
            nc.sync.dma_start(out=out_v[:, t, cols], in_=ob[:, i, cols])

        gate = const.tile([P, 1], U32, name="gate")
        tern_pos(0)
        tern_neg(0)
        x_quant(0, 0, 1)
        tern_sub(0)
        tern_pos(1)
        tw_quant(0)
        product(0, 0)
        product(1, 0)
        tern_neg(1)
        x_quant(0, 1, 1)
        product(2, 0)
        tern_sub(1)
        x_quant(0, 2, 2)
        tw_quant(1)
        nc.gpsimd.tensor_copy(out=gate[:], in_=twc[:, N - 1 : N])
        leave_sg(2, 0)
        product(3, 0)
        leave_sg(3, 0)
        for b in range(3):
            x_bank_t(1, b)
            x_bank_s(1, b)
        leave_v(0, 0)
        store_half(0, 0)
        leave_v(1, 0)
        store_half(1, 0)
        for t in range(3):
            product(t, 1)
        for t in range(2):
            leave_v(t, 1)
            store_half(t, 1)
        product(3, 1)
        product(4, 0)
        leave_v(2, 1)
        store(2, 1)
        product(4, 1)
        product(5, 0)
        leave_v(3, 1)
        store(3, 1)
        units = [(t, h) for t in range(4, MT) for h in range(2)]
        for n, (t, h) in enumerate(units):
            if 3 <= n + 2 < len(units):
                product(*units[n + 2])
            elif n + 2 == 2:
                pass
            if h == 0 and t % 2 == 0 and 4 <= t < 28:
                leave_sg(t, h)
            else:
                leave_v(t, h)
            if h == 1:
                if 4 <= t < 8-3:
                    x_bank_t(1, t - 4+3)
                    x_bank_s(1, t - 4+3)
                if t % 2 == 0 and TPC <= t < MT - TPC:
                    x_bank_t(1 + t // TPC, t % TPC // 2)
                    x_bank_s(1 + t // TPC, t % TPC // 2)
                if t % 8 == 5 and t < MT - TPC:
                    x_quant(1 + t // TPC, 0, 2)
                if t % 8 == 1 and t >= TPC:
                    x_quant(t // TPC, 2, 2)
                if t < 6 or t >= MT - 2:
                    store(t, 1)
                elif t % 2 == 1:
                    store(t - 1, 2)
